import numpy as np
import ml_dtypes


def mxq(x, axis, fmt="e4m3"):
    dtype, down = {"e4m3": (ml_dtypes.float8_e4m3fn, 7), "e5m2": (ml_dtypes.float8_e5m2, 14)}[fmt]
    v = np.moveaxis(np.asarray(x, np.float32).astype(ml_dtypes.bfloat16).astype(np.float64), axis, -1)
    blocks = v.reshape(v.shape[:-1] + (-1, 32))
    amax = np.abs(blocks).max(-1, keepdims=True)
    byte = np.maximum(np.where(amax > 0, np.frexp(amax)[1] - 1 + 127, 0) - down, 1)
    scale = np.exp2(byte - 127.0)
    codes = (blocks / scale).astype(np.float32).astype(dtype).astype(np.float64)
    return np.moveaxis((codes * scale).reshape(v.shape), -1, axis)


WIDE = False


def mx_kscale(k):
    if not WIDE:
        return np.ones(k)
    levels = np.array([18, -18])
    if k % 512:
        return np.exp2(np.random.permutation(np.resize(levels, k // 32))).repeat(32)
    a = np.empty((k // 512, 16))
    for p in range(k // 512):
        a[p, :8] = np.random.permutation(np.resize(levels, 8))
        for g in range(8):
            far = levels[np.abs(levels - a[p, g]) >= 10]
            a[p, g + 8] = far[np.random.randint(len(far))]
    return np.exp2(a.ravel()).repeat(32)


BF16 = ml_dtypes.bfloat16


def bf(x):
    return np.asarray(x, np.float32).astype(BF16)


def f64(x):
    return np.asarray(x).astype(np.float64)


BS, NF, N, J, NOUT = 2, 512, 512, 3, 512
KC = J * NF
EPS = 1e-5


def setup_inputs():
    u = mx_kscale(NOUT + NOUT)
    s = mx_kscale(N)
    s = s / np.max(s)
    v = mx_kscale(NF)
    t = np.tile(v, J)
    nb = N * np.random.choice([0.5, 0.625, 0.75, 0.875], BS)
    wt = np.random.choice([0.25, 0.5, 0.75, 1.0], (BS, 1, N))
    X0 = bf(np.random.standard_normal((BS, NF, N)))
    W0 = bf(np.random.standard_normal((BS, N, N, J)) / np.sqrt(N))
    cv1_w0 = bf(np.random.standard_normal((NOUT, KC)) / np.sqrt(KC))
    cv1_b = bf(np.random.standard_normal(NOUT) * 0.5)
    cv2_w0 = bf(np.random.standard_normal((NOUT, KC)) / np.sqrt(KC))
    cv2_b = bf(np.random.standard_normal(NOUT) * 0.5)
    bn_gamma = bf(1.0 + 0.1 * np.random.standard_normal(NOUT + NOUT))
    bn_beta = bf(0.3 * np.random.standard_normal(NOUT + NOUT))
    g = bf(4.0 * np.random.standard_normal((BS, NOUT + NOUT, N)) * np.exp2(np.random.randint(-6, 1, (BS, 1, N))) * u[None, :, None])
    x1 = f64(W0).transpose(0, 3, 1, 2) @ f64(X0).transpose(0, 2, 1)[:, None]
    x1 = x1.transpose(0, 1, 3, 2).reshape(BS, KC, N)
    z = np.concatenate([f64(cv2_w0) @ x1 + f64(cv2_b)[None, :, None], f64(cv1_w0) @ x1 + f64(cv1_b)[None, :, None]], axis=1)
    zb = np.maximum(z, 0.0)
    total = f64(bf(nb)).sum()
    mean = (zb * wt).sum(axis=(0, 2)) / total
    cz = zb - mean[None, :, None]
    rstd = 1.0 / np.sqrt((wt * cz * cz).sum(axis=(0, 2)) / total + EPS)
    return {"X": bf(f64(X0) / v[None, :, None]),
            "W": bf(f64(W0) / s[None, :, None, None]),
            "N_batch": bf(nb),
            "mask": bf(wt * s[None, None, :]),
            "cv1_w": bf(f64(cv1_w0) * t[None, :] / u[NOUT:, None]),
            "cv1_b": cv1_b,
            "cv2_w": bf(f64(cv2_w0) * t[None, :] / u[:NOUT, None]),
            "cv2_b": cv2_b,
            "bn_gamma": bn_gamma,
            "bn_beta": bn_beta,
            "z": np.asarray(z, np.float32),
            "mean": np.asarray(mean, np.float32),
            "rstd": np.asarray(rstd, np.float32),
            "grad_out": g}


def reference(X, W, N_batch, mask, cv1_w, cv1_b, cv2_w, cv2_b, bn_gamma, bn_beta, z, mean, rstd, grad_out):
    mk = f64(mask)
    zf = f64(z)
    r = f64(rstd)[None, :, None]
    total = f64(N_batch).sum()
    xh = (np.maximum(zf, 0.0) - f64(mean)[None, :, None]) * r
    dn = f64(grad_out) * mk * f64(bn_gamma)[None, :, None]
    a = (dn * xh).sum(axis=(0, 2))[None, :, None]
    dc = r * (dn - mk * xh * a / total)
    dzb = dc - mk * dc.sum(axis=(0, 2))[None, :, None] / total
    dz2 = np.where(zf > 0.0, dzb, 0.0)
    wc = np.concatenate([f64(cv2_w), f64(cv1_w)], axis=0)
    dx1 = mxq(wc, 0, "e4m3").T @ mxq(dz2, 1, "e5m2")
    d4 = dx1.reshape(BS, J, NF, N)
    dm = mxq(d4.transpose(0, 2, 1, 3).reshape(BS, NF, J * N), 2, "e5m2")
    wm = mxq(f64(W).transpose(0, 3, 1, 2).reshape(BS, J * N, N), 1, "e4m3")
    dX = dm @ wm
    df = mxq(d4, 2, "e5m2")
    xf = mxq(f64(X), 1, "e4m3")
    dW = df.transpose(0, 1, 3, 2) @ xf[:, None]
    return dX, dW.transpose(0, 2, 3, 1)

@@ -1,0 +1,561 @@
+from contextlib import ExitStack
+
+import concourse.mybir as mybir
+from concourse.masks import make_identity
+
+BS, NF, N, J, NOUT = 2, 512, 512, 3, 512
+FLOPS = 2 * BS * J * NF * N * (2 * NOUT + N + N)
+
+F32 = mybir.dt.float32
+BF16 = mybir.dt.bfloat16
+U32 = mybir.dt.uint32
+U8 = mybir.dt.uint8
+E4M3 = mybir.dt.float8_e4m3fn_x4
+E5M2 = mybir.dt.float8_e5m2_x4
+ALU = mybir.AluOpType
+ACT = mybir.ActivationFunctionType
+
+P = 128
+PACK = 4
+G = 2
+SLOTS = G * PACK
+STAGES = 4
+
+
+def tile_layer_simple_pa_v_kernel(
+    tc, X, W, N_batch, mask, cv1_w, cv1_b, cv2_w, cv2_b, bn_gamma, bn_beta, z, mean, rstd, grad_out, out_0, out_1
+):
+    nc = tc.nc
+    with ExitStack() as ctx:
+        sb = ctx.enter_context(tc.tile_pool(name="sb", bufs=1))
+        ps = ctx.enter_context(tc.psum_pool(name="ps", bufs=1))
+        ctx.enter_context(tc.manual_schedule())
+
+        def sbuf(name, shape, dtype, place=None):
+            return sb.tile([P] + shape, dtype, name=name, tag=place or name, align_bytes=64)
+
+        def psum(name, shape, dtype, bank):
+            return ps.tile([P] + shape, dtype, name=name, tag="bank%d" % bank)
+
+        turn = {"bank": 0, "stage": 0, "first": 3}
+
+        def next_bank(name, shape, dtype):
+            bank = turn["first"] + turn["bank"] % (8 - turn["first"])
+            turn["bank"] = turn["bank"] + 1
+            return psum(name, shape, dtype, bank)
+
+        def next_stage(name, width):
+            place = "stage%d" % (turn["stage"] % STAGES)
+            turn["stage"] = turn["stage"] + 1
+            return sbuf(name, [width], BF16, place)
+
+        def mx_pair(name, shape, place=None):
+            place = place or name
+            return sbuf(name + "_codes", shape, U32, place + "_c"), sbuf(name + "_scales", shape, U8, place + "_s")
+
+        def quantize(pair, where, src, fmt):
+            nc.vector.quantize_mx(out=pair[0][where].bitcast(fmt), scales=pair[1][where], in_=src)
+
+        def mx_pass(out, left, left_at, left_fmt, right, right_at, right_fmt, start, stop):
+            nc.tensor.matmul_mx(
+                out=out,
+                lhsT=left[0][left_at].bitcast(left_fmt),
+                lhsT_scale=left[1][left_at],
+                rhs=right[0][right_at].bitcast(right_fmt),
+                rhs_scale=right[1][right_at],
+                start=start,
+                stop=stop,
+            )
+
+        every = slice(None)
+
+        ident_bf = sbuf("ident_bf", [P], BF16)
+        make_identity(nc, ident_bf[:])
+        ident_f32 = sbuf("ident_f32", [P], F32)
+        make_identity(nc, ident_f32[:])
+
+        z_hbm = z.rearrange("b (g p s) m -> g s p b m", g=G, s=PACK)
+        g_hbm = grad_out.rearrange("b (g p h s) m -> g h p b s m", g=G, h=2, s=2)
+        wc_hbm = [w.rearrange("(p s) f -> p s f", s=PACK) for w in (cv2_w, cv1_w)]
+        z_sb, g_sb, wc_raw, w_raw, x_raw = {}, {}, {}, {}, {}
+
+        def load_z(k):
+            z_sb[k] = sbuf("z%d" % k, [BS, N], F32)
+            nc.sync.dma_start(out=z_sb[k][:], in_=z_hbm[k // PACK, k % PACK])
+
+        def load_g(k):
+            pair = sbuf("g%d" % k, [BS, 2, N], BF16)
+            nc.sync.dma_start(out=pair[:], in_=g_hbm[k // PACK, (k % PACK) // 2])
+            g_sb[k], g_sb[k + 1] = pair[:, :, 0, :], pair[:, :, 1, :]
+
+        def load_wc(g, j):
+            if j == 0:
+                wc_raw[g] = sbuf("wc_raw%d" % g, [PACK, J * NF], BF16, "big%d" % g)
+            cols = slice(j * NF, (j + 1) * NF)
+            nc.sync.dma_start(out=wc_raw[g][:, :, cols], in_=wc_hbm[g][:, :, cols])
+
+        def load_x(b):
+            x_raw[b] = sbuf("x_raw%d" % b, [PACK, N], BF16)
+            nc.sync.dma_start(out=x_raw[b][:], in_=X[b].rearrange("(p t) n -> p t n", t=PACK))
+
+        def load_w(b):
+            w_raw[b] = sbuf("w_raw%d" % b, [PACK, N * J], BF16, "big%d" % (2 if b == 0 else 0))
+            nc.sync.dma_start(out=w_raw[b][:], in_=W[b].rearrange("(p t) n j -> p t (n j)", t=PACK))
+
+        mask8 = sbuf("mask8", [8], BF16)
+        nc.sync.dma_start(out=mask8[:], in_=mask.rearrange("b o (q e) -> (b o q) e", e=8))
+        load_z(0)
+        load_z(1)
+        load_g(0)
+        load_z(2)
+        load_g(2)
+        load_z(3)
+        load_wc(0, 0)
+        gamma_sb = sbuf("gamma_sb", [G, PACK], BF16)
+        mean_sb = sbuf("mean_sb", [G, PACK], F32)
+        rstd_sb = sbuf("rstd_sb", [G, PACK], F32)
+        count_sb = sbuf("count_sb", [BS], BF16)
+        nc.sync.dma_start(out=count_sb[:], in_=N_batch.partition_broadcast(P))
+        for tile, vec in ((gamma_sb, bn_gamma), (mean_sb, mean), (rstd_sb, rstd)):
+            nc.sync.dma_start(out=tile[:], in_=vec.rearrange("(g p s) -> p g s", g=G, s=PACK))
+        load_z(4)
+        load_g(4)
+        load_z(5)
+        load_wc(0, 1)
+        load_z(6)
+        load_g(6)
+        load_z(7)
+        load_wc(0, 2)
+        for j in range(J):
+            load_wc(1, j)
+        load_x(0)
+        load_w(0)
+        load_x(1)
+
+        def mask_in_psum(tile):
+            for e in range(8):
+                nc.tensor.transpose(tile[:, e, :], mask8[:, e : e + 1].to_broadcast([P, P]), ident_bf[:])
+            return tile[:].rearrange("p e q -> p q e")
+
+        mask_row_ps = mask_in_psum(psum("mask_ps", [8, P], BF16, 0))
+        mask_row = sbuf("mask_row", [BS * N], BF16)
+        mask_sum = sbuf("mask_sum", [1], F32)
+        mask_col = sbuf("mask_col", [8], BF16)
+
+        def spread_mask():
+            nc.scalar.activation(
+                out=mask_row[:].rearrange("p (q e) -> p q e", e=8), in_=mask_in_psum(next_bank("mask_ps2", [8, P], BF16)), func=ACT.Identity, accum_out=mask_sum[:]
+            )
+            cols = next_bank("mask_cols", [8, P], BF16)
+            for blk in range(8):
+                nc.tensor.transpose(cols[:, blk, :], mask_row[:, blk * P : (blk + 1) * P], ident_bf[:])
+            nc.scalar.copy(out=mask_col[:], in_=cols[:, :, 0])
+
+        sum_zm = sbuf("sum_zm", [SLOTS], F32)
+        sum_gzm = sbuf("sum_gzm", [SLOTS], F32)
+        sum_gm = [psum("sum_gm%d" % g, [PACK], F32, 1 + g) for g in range(G)]
+        gate = [sbuf("gate%d" % g, [BS, PACK, N], BF16) for g in range(G)]
+        unread = sbuf("unread", [BS, N], F32, "dx_b0_j2")
+        zm, g_t = {}, {}
+
+        def relu_mask(k):
+            zm[k] = sbuf("zm%d" % k, [BS, N], F32, "zm%d" % (k % 3))
+            nc.vector.scalar_tensor_tensor(
+                out=zm[k][:].rearrange("p b (q e) -> p (b q) e", e=8),
+                in0=z_sb[k][:].rearrange("p b (q e) -> p (b q) e", e=8),
+                scalar=0.0,
+                in1=mask_row_ps,
+                op0=ALU.max,
+                op1=ALU.mult,
+                accum_out=sum_zm[:, k : k + 1],
+            )
+
+        def sign_of(k):
+            nc.scalar.activation(out=gate[k // PACK][:, :, k % PACK, :], in_=zm[k][:], func=ACT.Sign)
+
+        def dot_g(k):
+            nc.vector.scalar_tensor_tensor(
+                out=unread[:], in0=zm[k][:], scalar=1.0, in1=g_sb[k], op0=ALU.mult, op1=ALU.mult, accum_out=sum_gzm[:, k : k + 1]
+            )
+
+        def transpose_g(k):
+            turned = next_bank("g_turned%d" % k, [8, P], BF16)
+            for blk in range(8):
+                b, mt = divmod(blk, 4)
+                nc.tensor.transpose(turned[:, blk, :], g_sb[k][:, b, mt * P : (mt + 1) * P], ident_bf[:])
+            g_t[k] = sbuf("g_t%d" % k, [8, P], BF16, "g_t%d" % (k % 2))
+            nc.scalar.copy(out=g_t[k][:], in_=turned[:])
+
+        def sum_g(k):
+            g, s = divmod(k, PACK)
+            for blk in range(8):
+                nc.tensor.matmul(
+                    sum_gm[g][:, s : s + 1], lhsT=g_t[k][:, blk, :], rhs=mask_col[:, blk : blk + 1], start=(blk == 0), stop=(blk == 7)
+                )
+
+        def small(name, width=SLOTS):
+            return sbuf(name, [width], F32)
+
+        gamma_f = gamma_sb[:].rearrange("p g s -> p (g s)")
+        mean_f = mean_sb[:].rearrange("p g s -> p (g s)")
+        rstd_f = rstd_sb[:].rearrange("p g s -> p (g s)")
+        total, inv_total, share = small("total", 1), small("inv_total", 1), small("share", 1)
+        coef_a, a_over_total, rstd_sq, neg_k, mean_rest = (small(n) for n in ("coef_a", "a_over_total", "rstd_sq", "neg_k", "mean_rest"))
+        q1, q2, q3, q4, q5, neg_b, coef_c = (small(n) for n in ("q1", "q2", "q3", "q4", "q5", "neg_b", "coef_c"))
+        V = nc.vector
+
+        const_steps = [
+            [
+                lambda: V.tensor_reduce(out=total[:], in_=count_sb[:], axis=mybir.AxisListType.X, op=ALU.add),
+                lambda: V.tensor_tensor(out=coef_a[:], in0=rstd_f, in1=gamma_f, op=ALU.mult),
+                lambda: V.tensor_tensor(out=rstd_sq[:], in0=rstd_f, in1=rstd_f, op=ALU.mult),
+            ],
+            [lambda: V.reciprocal(out=inv_total[:], in_=total[:])],
+            [
+                lambda: V.tensor_scalar(out=a_over_total[:], in0=coef_a[:], scalar1=inv_total[:], scalar2=None, op0=ALU.mult),
+                lambda: V.tensor_scalar(out=share[:], in0=mask_sum[:], scalar1=inv_total[:], scalar2=-1.0, op0=ALU.mult, op1=ALU.mult),
+            ],
+            [
+                lambda: V.scalar_tensor_tensor(out=neg_k[:], in0=rstd_sq[:], scalar=-1.0, in1=a_over_total[:], op0=ALU.mult, op1=ALU.mult),
+                lambda: V.scalar_tensor_tensor(out=mean_rest[:], in0=mean_f, scalar=share[:], in1=mean_f, op0=ALU.mult, op1=ALU.add),
+            ],
+        ]
+
+        def stat_steps(g):
+            c = slice(g * PACK, (g + 1) * PACK)
+            return [
+                [
+                    lambda: V.tensor_tensor(out=q1[:, c], in0=mean_f[:, c], in1=sum_gm[g][:], op=ALU.mult),
+                    lambda: V.tensor_tensor(out=q4[:, c], in0=a_over_total[:, c], in1=sum_gm[g][:], op=ALU.mult),
+                    lambda: V.scalar_tensor_tensor(
+                        out=q3[:, c], in0=sum_zm[:, c], scalar=inv_total[:], in1=mean_rest[:, c], op0=ALU.mult, op1=ALU.add
+                    ),
+                ],
+                [lambda: V.tensor_tensor(out=q2[:, c], in0=sum_gzm[:, c], in1=q1[:, c], op=ALU.subtract)],
+                [lambda: V.tensor_tensor(out=neg_b[:, c], in0=q2[:, c], in1=neg_k[:, c], op=ALU.mult)],
+                [lambda: V.tensor_tensor(out=q5[:, c], in0=neg_b[:, c], in1=q3[:, c], op=ALU.mult)],
+                [
+                    lambda: V.scalar_tensor_tensor(
+                        out=coef_c[:, c], in0=q5[:, c], scalar=-1.0, in1=q4[:, c], op0=ALU.mult, op1=ALU.subtract
+                    )
+                ],
+            ]
+
+        def run(steps):
+            for step in steps:
+                step()
+
+        affine, dz_bf, dz_stage = {}, {}, {}
+        dz_mx = mx_pair("dz", [BS, G, N])
+
+        def affine_z(g, b):
+            affine[g, b] = sbuf("affine%d%d" % (g, b), [PACK, N], F32, "affine%d" % g)
+            for s in range(PACK):
+                k = g * PACK + s
+                nc.scalar.activation(
+                    out=affine[g, b][:, s, :], in_=z_sb[k][:, b, :], func=ACT.Identity, scale=neg_b[:, k : k + 1], bias=coef_c[:, k : k + 1]
+                )
+
+        def weigh_gate(g, b):
+            row = mask_row[:, b * N : (b + 1) * N].unsqueeze(1).to_broadcast([P, PACK, N])
+            V.tensor_tensor(out=gate[g][:, b, :, :], in0=gate[g][:, b, :, :], in1=row, op=ALU.mult)
+
+        def add_g(g, b, s):
+            k = g * PACK + s
+            V.scalar_tensor_tensor(
+                out=affine[g, b][:, s, :], in0=g_sb[k][:, b, :], scalar=coef_a[:, k : k + 1], in1=affine[g, b][:, s, :], op0=ALU.mult, op1=ALU.add
+            )
+
+        def round_dz(g, b):
+            dz_bf[g, b] = sbuf("dz_bf%d%d" % (g, b), [PACK, N], BF16, "dz_bf%d" % g)
+            V.tensor_tensor(out=dz_bf[g, b][:], in0=affine[g, b][:], in1=gate[g][:, b, :, :], op=ALU.mult)
+
+        def group_dz(g, b):
+            dz_stage[g, b] = next_stage("dz_stage%d%d" % (g, b), PACK * N)
+            V.tensor_copy(
+                out=dz_stage[g, b][:].rearrange("p (t x i s) -> p x t i s", t=PACK, i=2, s=PACK),
+                in_=dz_bf[g, b][:].rearrange("p s (x i t) -> p x t i s", i=2, t=PACK),
+            )
+
+        def quantize_dz(g, b):
+            quantize(dz_mx, (every, b, g, every), dz_stage[g, b][:], E5M2)
+
+        wc_mx = mx_pair("wc", [G, J, NF])
+        w_mx = mx_pair("w", [BS, J, N])
+        x_mx = mx_pair("x", [BS, N])
+        staged = {}
+
+        def group_on_scalar(key, src):
+            staged[key] = next_stage("st_" + key, PACK * N)
+            nc.scalar.copy(
+                out=staged[key][:].rearrange("p (c i t) -> p c t i", i=4, t=PACK), in_=src.rearrange("p t (c i) -> p c t i", i=4)
+            )
+
+        def group_on_tensor(key, src):
+            staged[key] = next_stage("st_" + key, PACK * N)
+            for half in range(2):
+                bank = next_bank("grp_%s_%d" % (key, half), [2, P, PACK], BF16)
+                for q in range(2):
+                    cols = slice((2 * half + q) * P, (2 * half + q + 1) * P)
+                    nc.tensor.matmul(bank[:, q, :, :], lhsT=ident_bf[:], rhs=src[:, :, cols].rearrange("p t c -> p c t"), start=True, stop=True)
+                nc.scalar.copy(out=staged[key][:, half * 1024 : (half + 1) * 1024], in_=bank[:].rearrange("p q c t -> p (q c t)"))
+
+        def group_wc(g, j):
+            src = wc_raw[g][:, :, j * NF : (j + 1) * NF]
+            (group_on_tensor if (g, j) == (G - 1, J - 1) else group_on_scalar)("wc%d%d" % (g, j), src)
+
+        def quantize_wc(g, j):
+            quantize(wc_mx, (every, g, j, every), staged["wc%d%d" % (g, j)][:], E4M3)
+
+        def group_x(b):
+            group_on_tensor("x%d" % b, x_raw[b][:])
+
+        def quantize_x(b):
+            quantize(x_mx, (every, b, every), staged["x%d" % b][:], E4M3)
+
+        def group_w(b, j):
+            group_on_tensor("w%d%d" % (b, j), w_raw[b][:].rearrange("p t (n j) -> p j t n", j=J)[:, j, :, :])
+
+        def quantize_w(b, j):
+            quantize(w_mx, (every, b, j, every), staged["w%d%d" % (b, j)][:], E4M3)
+
+        dx_bf, f_stage, f_mx, dw_sb, dx_ps, dw_ps, word_ps, m_mx = {}, {}, {}, {}, {}, {}, {}, {}
+        dw_hbm = out_1.rearrange("b (p t) n j -> b t p (n j)", t=PACK)
+        dxo_hbm = out_0.rearrange("b (p c) n -> b c p n", c=PACK)
+
+        def first_product(i):
+            b, t = divmod(i, PACK)
+            for j in range(J):
+                dx_ps[i, j] = next_bank("dx_ps%d%d" % (i, j), [NF], F32)
+                for g in range(G):
+                    mx_pass(
+                        dx_ps[i, j][:], dz_mx, (every, b, g, slice(t * P, (t + 1) * P)), E5M2, wc_mx, (every, g, j, every), E4M3, g == 0, g == G - 1
+                    )
+
+        def round_dx(i, j, eng):
+            b, t = divmod(i, PACK)
+            if t == 0:
+                dx_bf[b, j] = sbuf("dx_bf%d%d" % (b, j), [PACK, NF], BF16, "dx_b0_j%d" % j if b == 0 else "z%d" % j)
+            out = dx_bf[b, j][:, t, :].rearrange("p (u w e) -> p u w e", u=2, e=2)
+            eng(out=out, in_=dx_ps[i, j][:].rearrange("p (w u e) -> p u w e", u=2, e=2))
+
+        def turn_words(i):
+            b, t = divmod(i, PACK)
+            word_ps[i] = [next_bank("word_ps%d_0" % i, [2, 2, P], F32), next_bank("word_ps%d_1" % i, [1, 2, P], F32)]
+            for j in range(J):
+                words = dx_bf[b, j][:, t, :].bitcast(F32)
+                for u in range(2):
+                    nc.tensor.transpose(word_ps[i][j // 2][:, j % 2, u, :], words[:, u * P : (u + 1) * P], ident_f32[:])
+
+        def group_words(i, part, eng):
+            if part == 0:
+                f_stage[i] = next_stage("f_stage%d" % i, J * NF)
+            cols = (slice(0, 2 * NF), slice(2 * NF, 3 * NF))[part]
+            out = f_stage[i][:, cols].bitcast(F32).rearrange("p (j x u) -> p j x u", x=P, u=2)
+            eng(out=out, in_=word_ps[i][part][:].rearrange("p j u x -> p j x u"))
+
+        def quantize_f(i):
+            f_mx[i] = mx_pair("f%d" % i, [J * P], "f%d" % (i % 2))
+            quantize(f_mx[i], (every, slice(0, 2 * P)), f_stage[i][:, 0 : 2 * NF], E5M2)
+            quantize(f_mx[i], (every, slice(2 * P, 3 * P)), f_stage[i][:, 2 * NF : 3 * NF], E5M2)
+
+        def dw_product(i):
+            for j in range(J):
+                dw_ps[i, j] = next_bank("dw_ps%d%d" % (i, j), [N], F32)
+                mx_pass(dw_ps[i, j][:], f_mx[i], (every, slice(j * P, (j + 1) * P)), E5M2, x_mx, (every, i // PACK, every), E4M3, True, True)
+
+        def dw_out(i, j, eng):
+            if j == 0:
+                dw_sb[i] = sbuf("dw_sb%d" % i, [2, J * N], F32, "big%d" % ((1 + i) % 3))
+            eng(out=dw_sb[i][:, 0, j * N : (j + 1) * N], in_=dw_ps[i, j][:])
+
+        def dw_store(i):
+            V.tensor_copy(
+                out=dw_sb[i][:, 1, :].rearrange("p (c i j) -> p c j i", i=4, j=J), in_=dw_sb[i][:, 0, :].rearrange("p (j c i) -> p c j i", j=J, i=4)
+            )
+            nc.sync.dma_start(out=dw_hbm[i // PACK, i % PACK], in_=dw_sb[i][:, 1, :])
+
+        def group_m(b, j, *engines):
+            key = "m%d%d" % (b, j)
+            staged[key] = next_stage("st_" + key, PACK * NF)
+            for u in range(2):
+                engines[u % len(engines)](
+                    out=staged[key][:, u * 1024 : (u + 1) * 1024].rearrange("p (e y i t) -> p y e i t", e=2, i=4, t=PACK),
+                    in_=dx_bf[b, j][:, :, u * 256 : (u + 1) * 256].rearrange("p t (y i e) -> p y e i t", i=4, e=2),
+                )
+
+        def quantize_m(b, j):
+            if j == 0:
+                m_mx[b] = mx_pair("m%d" % b, [J, NF], "m" if b == 0 else "wc")
+            quantize(m_mx[b], (every, j, every), staged["m%d%d" % (b, j)][:], E5M2)
+
+        dxo_ps = {}
+
+        def dx_product(b, j):
+            for c in range(PACK):
+                if j == 0:
+                    dxo_ps[b, c] = next_bank("dxo_ps%d%d" % (b, c), [N], F32)
+                mx_pass(dxo_ps[b, c][:], m_mx[b], (every, j, slice(c * P, (c + 1) * P)), E5M2, w_mx, (every, b, j, every), E4M3, j == 0, j == J - 1)
+
+        def dx_tile(b, c):
+            dxo_ps[b, c] = next_bank("dxo_ps%d%d" % (b, c), [N], F32)
+            for j in range(J):
+                mx_pass(dxo_ps[b, c][:], m_mx[b], (every, j, slice(c * P, (c + 1) * P)), E5M2, w_mx, (every, b, j, every), E4M3, j == 0, j == J - 1)
+
+        def dx_store(b, c, eng):
+            res = sbuf("dxo%d%d" % (b, c), [N], F32, ("zm0", "zm1", "zm2", "g_t0")[c])
+            eng(out=res[:], in_=dxo_ps[b, c][:])
+            nc.sync.dma_start(out=dxo_hbm[b, c], in_=res[:])
+
+        S = nc.scalar.copy
+        VC = nc.vector.tensor_copy
+
+        stats0, stats1 = stat_steps(0), stat_steps(1)
+        after_relu = {4: const_steps[0], 5: const_steps[2], 6: stats0[0], 7: stats0[2]}
+        after_dot = {4: const_steps[1], 5: const_steps[3], 6: stats0[1], 7: stats0[3]}
+        relu_mask(0)
+        spread_mask()
+        sign_of(0)
+        transpose_g(0)
+        for k in range(1, SLOTS):
+            relu_mask(k)
+            sign_of(k)
+            transpose_g(k)
+            sum_g(k - 1)
+            run(after_relu.get(k, []))
+            if k in (4, 6):
+                group_wc(0, k // 6)
+            dot_g(k - 1)
+            run(after_dot.get(k, []))
+            if k == 6:
+                quantize_wc(0, 0)
+        sum_g(SLOTS - 1)
+        quantize_wc(0, 1)
+        run(stats0[4])
+        affine_z(0, 0)
+        dot_g(SLOTS - 1)
+        run(stats1[0])
+        weigh_gate(0, 0)
+        run(stats1[1])
+        group_wc(0, 2)
+        add_g(0, 0, 0)
+        run(stats1[2])
+        add_g(0, 0, 1)
+        run(stats1[3])
+        add_g(0, 0, 2)
+        run(stats1[4])
+        affine_z(1, 0)
+        add_g(0, 0, 3)
+        weigh_gate(1, 0)
+        group_wc(1, 0)
+        load_w(1)
+        round_dz(0, 0)
+        quantize_wc(0, 2)
+        group_dz(0, 0)
+        group_wc(1, 1)
+        for s in range(PACK):
+            add_g(1, 0, s)
+        quantize_dz(0, 0)
+        quantize_wc(1, 0)
+        group_wc(1, 2)
+        round_dz(1, 0)
+        quantize_wc(1, 1)
+        affine_z(0, 1)
+        group_dz(1, 0)
+        quantize_wc(1, 2)
+        group_x(0)
+        quantize_dz(1, 0)
+        turn["first"], turn["bank"] = 0, 0
+
+        def step(i, first=(S, S, S), words=(S, S), second=(S, S, S)):
+            if i < 8:
+                first_product(i)
+            if 1 <= i < 9:
+                turn_words(i - 1)
+            if 2 <= i:
+                dw_product(i - 2)
+            if i < 8:
+                for j in range(J):
+                    round_dx(i, j, first[j])
+            if 1 <= i < 9:
+                group_words(i - 1, 0, words[0])
+                group_words(i - 1, 1, words[1])
+            if 2 <= i:
+                for j in range(J):
+                    dw_out(i - 2, j, second[j])
+
+        group_w(0, 0)
+        step(0)
+        quantize_x(0)
+        weigh_gate(0, 1)
+        quantize_w(0, 0)
+        group_w(0, 1)
+        group_w(0, 2)
+        for s in range(PACK):
+            add_g(0, 1, s)
+        affine_z(1, 1)
+        quantize_w(0, 1)
+        weigh_gate(1, 1)
+        step(1)
+        round_dz(0, 1)
+        quantize_w(0, 2)
+        group_dz(0, 1)
+        quantize_f(0)
+        group_x(1)
+        step(2)
+        for s in range(PACK):
+            add_g(1, 1, s)
+        quantize_dz(0, 1)
+        quantize_f(1)
+        group_w(1, 0)
+        round_dz(1, 1)
+        quantize_x(1)
+        step(3)
+        group_dz(1, 1)
+        dw_store(0)
+        quantize_dz(1, 1)
+        quantize_f(2)
+        group_w(1, 1)
+        quantize_w(1, 0)
+        group_w(1, 2)
+        dw_store(1)
+        quantize_w(1, 1)
+        step(4)
+        quantize_w(1, 2)
+        group_m(0, 0, VC)
+        quantize_f(3)
+        quantize_m(0, 0)
+        group_m(0, 1, VC)
+        dw_store(2)
+        quantize_m(0, 1)
+        step(5)
+        group_m(0, 2, VC)
+        quantize_f(4)
+        quantize_m(0, 2)
+        dw_store(3)
+        step(6, words=(VC, VC))
+        quantize_f(5)
+        for c in range(PACK):
+            dx_tile(0, c)
+            if c == 0:
+                dw_store(4)
+            dx_store(0, c, VC)
+        step(7, first=(S, VC, S), words=(VC, S))
+        quantize_f(6)
+        group_m(1, 0, VC)
+        dw_store(5)
+        step(8)
+        quantize_m(1, 0)
+        quantize_f(7)
+        group_m(1, 1, VC)
+        dw_store(6)
+        quantize_m(1, 1)
+        step(9)
+        group_m(1, 2, VC, S)
+        dw_store(7)
+        dx_product(1, 0)
+        dx_product(1, 1)
+        quantize_m(1, 2)
+        dx_product(1, 2)
+        for c in range(PACK):
+            dx_store(1, c, VC if c % 2 else S)

@@ -69,10 +69,10 @@ def tile_layer_simple_pa_v_kernel(
 
         every = slice(None)
 
-        ident_bf = sbuf("ident_bf", [P], BF16)
-        make_identity(nc, ident_bf[:])
         ident_f32 = sbuf("ident_f32", [P], F32)
         make_identity(nc, ident_f32[:])
+        ident_bf = sbuf("ident_bf", [P], BF16)
+        make_identity(nc, ident_bf[:])
 
         z_hbm = z.rearrange("b (g p s) m -> g s p b m", g=G, s=PACK)
         g_hbm = grad_out.rearrange("b (g p h s) m -> g h p b s m", g=G, h=2, s=2)
@@ -102,8 +102,8 @@ def tile_layer_simple_pa_v_kernel(
             w_raw[b] = sbuf("w_raw%d" % b, [PACK, N * J], BF16, "big%d" % (2 if b == 0 else 0))
             nc.sync.dma_start(out=w_raw[b][:], in_=W[b].rearrange("(p t) n j -> p t (n j)", t=PACK))
 
-        mask8 = sbuf("mask8", [8], BF16)
-        nc.sync.dma_start(out=mask8[:], in_=mask.rearrange("b o (q e) -> (b o q) e", e=8))
+        mask_col = sbuf("mask_col", [4, 2], BF16)
+        nc.sync.dma_start(out=mask_col[:], in_=mask.rearrange("b o (h w e) -> w (b o h) e", h=2, e=2))
         load_z(0)
         load_z(1)
         load_g(0)
@@ -133,23 +133,19 @@ def tile_layer_simple_pa_v_kernel(
         load_x(1)
 
         def mask_in_psum(tile):
-            for e in range(8):
-                nc.tensor.transpose(tile[:, e, :], mask8[:, e : e + 1].to_broadcast([P, P]), ident_bf[:])
-            return tile[:].rearrange("p e q -> p q e")
+            words = mask_col[:].rearrange("p k e -> p (k e)").bitcast(F32)
+            for blk in range(4):
+                nc.tensor.transpose(tile[:, blk, :], words[:, blk : blk + 1].to_broadcast([P, P]), ident_f32[:])
+            return tile[:].rearrange("p k w -> p (k w)").bitcast(BF16)
 
-        mask_row_ps = mask_in_psum(psum("mask_ps", [8, P], BF16, 0))
+        mask_row_ps = mask_in_psum(psum("mask_ps", [4, P], F32, 0))
         mask_row = sbuf("mask_row", [BS * N], BF16)
         mask_sum = sbuf("mask_sum", [1], F32)
-        mask_col = sbuf("mask_col", [8], BF16)
 
         def spread_mask():
             nc.scalar.activation(
-                out=mask_row[:].rearrange("p (q e) -> p q e", e=8), in_=mask_in_psum(next_bank("mask_ps2", [8, P], BF16)), func=ACT.Identity, accum_out=mask_sum[:]
+                out=mask_row[:], in_=mask_in_psum(next_bank("mask_ps2", [4, P], F32)), func=ACT.Identity, accum_out=mask_sum[:]
             )
-            cols = next_bank("mask_cols", [8, P], BF16)
-            for blk in range(8):
-                nc.tensor.transpose(cols[:, blk, :], mask_row[:, blk * P : (blk + 1) * P], ident_bf[:])
-            nc.scalar.copy(out=mask_col[:], in_=cols[:, :, 0])
 
         sum_zm = sbuf("sum_zm", [SLOTS], F32)
         sum_gzm = sbuf("sum_gzm", [SLOTS], F32)
@@ -161,8 +157,8 @@ def tile_layer_simple_pa_v_kernel(
         def relu_mask(k):
             zm[k] = sbuf("zm%d" % k, [BS, N], F32, "zm%d" % (k % 3))
             nc.vector.scalar_tensor_tensor(
-                out=zm[k][:].rearrange("p b (q e) -> p (b q) e", e=8),
-                in0=z_sb[k][:].rearrange("p b (q e) -> p (b q) e", e=8),
+                out=zm[k][:].rearrange("p b m -> p (b m)"),
+                in0=z_sb[k][:].rearrange("p b m -> p (b m)"),
                 scalar=0.0,
                 in1=mask_row_ps,
                 op0=ALU.max,
@@ -179,18 +175,19 @@ def tile_layer_simple_pa_v_kernel(
             )
 
         def transpose_g(k):
-            turned = next_bank("g_turned%d" % k, [8, P], BF16)
-            for blk in range(8):
-                b, mt = divmod(blk, 4)
-                nc.tensor.transpose(turned[:, blk, :], g_sb[k][:, b, mt * P : (mt + 1) * P], ident_bf[:])
-            g_t[k] = sbuf("g_t%d" % k, [8, P], BF16, "g_t%d" % (k % 2))
-            nc.scalar.copy(out=g_t[k][:], in_=turned[:])
+            turned = next_bank("g_turned%d" % k, [4, P], F32)
+            for blk in range(4):
+                b, h = divmod(blk, 2)
+                nc.tensor.transpose(turned[:, blk, :], g_sb[k][:, b, :].bitcast(F32)[:, h * P : (h + 1) * P], ident_f32[:])
+            g_t[k] = sbuf("g_t%d" % k, [4, P, 2], BF16, "g_t%d" % (k % 2))
+            nc.scalar.copy(out=g_t[k][:].rearrange("p k c e -> p (k c e)").bitcast(F32), in_=turned[:].rearrange("p k c -> p (k c)"))
 
         def sum_g(k):
             g, s = divmod(k, PACK)
-            for blk in range(8):
+            for step in range(8):
+                blk, e = divmod(step, 2)
                 nc.tensor.matmul(
-                    sum_gm[g][:, s : s + 1], lhsT=g_t[k][:, blk, :], rhs=mask_col[:, blk : blk + 1], start=(blk == 0), stop=(blk == 7)
+                    sum_gm[g][:, s : s + 1], lhsT=g_t[k][:, blk, :, e], rhs=mask_col[:, blk, e : e + 1], start=(step == 0), stop=(step == 7)
                 )
 
         def small(name, width=SLOTS):
@@ -291,14 +288,23 @@ def tile_layer_simple_pa_v_kernel(
                 out=staged[key][:].rearrange("p (c i t) -> p c t i", i=4, t=PACK), in_=src.rearrange("p t (c i) -> p c t i", i=4)
             )
 
+        grouped_ps = {}
+
         def group_on_tensor(key, src):
+            grouped_ps[key] = [next_bank("grp_%s_%d" % (key, half), [2, P, PACK], BF16) for half in range(2)]
+            for q in range(4):
+                nc.tensor.matmul(
+                    grouped_ps[key][q // 2][:, q % 2, :, :].rearrange("p (c i) t -> p c t i", i=8),
+                    lhsT=ident_bf[:],
+                    rhs=src[:, :, q * P : (q + 1) * P].rearrange("p t (c i) -> p c t i", i=8),
+                    start=True,
+                    stop=True,
+                )
+
+        def fetch_grouped(key):
             staged[key] = next_stage("st_" + key, PACK * N)
             for half in range(2):
-                bank = next_bank("grp_%s_%d" % (key, half), [2, P, PACK], BF16)
-                for q in range(2):
-                    cols = slice((2 * half + q) * P, (2 * half + q + 1) * P)
-                    nc.tensor.matmul(bank[:, q, :, :], lhsT=ident_bf[:], rhs=src[:, :, cols].rearrange("p t c -> p c t"), start=True, stop=True)
-                nc.scalar.copy(out=staged[key][:, half * 1024 : (half + 1) * 1024], in_=bank[:].rearrange("p q c t -> p (q c t)"))
+                nc.scalar.copy(out=staged[key][:, half * 1024 : (half + 1) * 1024], in_=grouped_ps[key][half][:].rearrange("p q c t -> p (q c t)"))
 
         def group_wc(g, j):
             src = wc_raw[g][:, :, j * NF : (j + 1) * NF]
@@ -369,8 +375,8 @@ def tile_layer_simple_pa_v_kernel(
                 dw_sb[i] = sbuf("dw_sb%d" % i, [2, J * N], F32, "big%d" % ((1 + i) % 3))
             eng(out=dw_sb[i][:, 0, j * N : (j + 1) * N], in_=dw_ps[i, j][:])
 
-        def dw_store(i):
-            V.tensor_copy(
+        def dw_store(i, eng=nc.vector.tensor_copy):
+            eng(
                 out=dw_sb[i][:, 1, :].rearrange("p (c i j) -> p c j i", i=4, j=J), in_=dw_sb[i][:, 0, :].rearrange("p (j c i) -> p c j i", j=J, i=4)
             )
             nc.sync.dma_start(out=dw_hbm[i // PACK, i % PACK], in_=dw_sb[i][:, 1, :])
@@ -403,7 +409,7 @@ def tile_layer_simple_pa_v_kernel(
                 mx_pass(dxo_ps[b, c][:], m_mx[b], (every, j, slice(c * P, (c + 1) * P)), E5M2, w_mx, (every, b, j, every), E4M3, j == 0, j == J - 1)
 
         def dx_store(b, c, eng):
-            res = sbuf("dxo%d%d" % (b, c), [N], F32, ("zm0", "zm1", "zm2", "g_t0")[c])
+            res = sbuf("dxo%d%d" % (b, c), [N], F32, ("zm0", "zm1", "zm2", "z3", "z4", "z5", "z6", "z7")[b * PACK + c])
             eng(out=res[:], in_=dxo_ps[b, c][:])
             nc.sync.dma_start(out=dxo_hbm[b, c], in_=res[:])
 
@@ -434,18 +440,23 @@ def tile_layer_simple_pa_v_kernel(
         run(stats0[4])
         affine_z(0, 0)
         dot_g(SLOTS - 1)
-        run(stats1[0])
         weigh_gate(0, 0)
-        run(stats1[1])
+        run(stats1[0])
+        turn["first"], turn["bank"] = 0, 3
+        group_wc(1, 2)
+        group_x(0)
+        group_w(0, 0)
+        group_w(0, 1)
         group_wc(0, 2)
         add_g(0, 0, 0)
-        run(stats1[2])
+        run(stats1[1])
         add_g(0, 0, 1)
-        run(stats1[3])
+        run(stats1[2])
         add_g(0, 0, 2)
+        run(stats1[3])
+        add_g(0, 0, 3)
         run(stats1[4])
         affine_z(1, 0)
-        add_g(0, 0, 3)
         weigh_gate(1, 0)
         group_wc(1, 0)
         load_w(1)
@@ -457,15 +468,22 @@ def tile_layer_simple_pa_v_kernel(
             add_g(1, 0, s)
         quantize_dz(0, 0)
         quantize_wc(1, 0)
-        group_wc(1, 2)
+        fetch_grouped("wc12")
+        group_w(0, 2)
         round_dz(1, 0)
         quantize_wc(1, 1)
         affine_z(0, 1)
         group_dz(1, 0)
         quantize_wc(1, 2)
-        group_x(0)
+        fetch_grouped("x0")
+        group_x(1)
+        fetch_grouped("w00")
+        group_w(1, 0)
         quantize_dz(1, 0)
-        turn["first"], turn["bank"] = 0, 0
+        fetch_grouped("w01")
+        quantize_x(0)
+        quantize_w(0, 0)
+        fetch_grouped("w02")
 
         def step(i, first=(S, S, S), words=(S, S), second=(S, S, S)):
             if i < 8:
@@ -484,44 +502,41 @@ def tile_layer_simple_pa_v_kernel(
                 for j in range(J):
                     dw_out(i - 2, j, second[j])
 
-        group_w(0, 0)
         step(0)
-        quantize_x(0)
         weigh_gate(0, 1)
-        quantize_w(0, 0)
-        group_w(0, 1)
-        group_w(0, 2)
+        fetch_grouped("x1")
+        quantize_w(0, 1)
+        fetch_grouped("w10")
+        group_w(1, 1)
         for s in range(PACK):
             add_g(0, 1, s)
         affine_z(1, 1)
-        quantize_w(0, 1)
+        quantize_w(0, 2)
         weigh_gate(1, 1)
         step(1)
+        quantize_x(1)
+        fetch_grouped("w11")
+        group_w(1, 2)
         round_dz(0, 1)
-        quantize_w(0, 2)
+        quantize_w(1, 0)
+        fetch_grouped("w12")
         group_dz(0, 1)
         quantize_f(0)
-        group_x(1)
         step(2)
+        quantize_w(1, 1)
         for s in range(PACK):
             add_g(1, 1, s)
         quantize_dz(0, 1)
         quantize_f(1)
-        group_w(1, 0)
         round_dz(1, 1)
-        quantize_x(1)
+        quantize_w(1, 2)
         step(3)
         group_dz(1, 1)
         dw_store(0)
         quantize_dz(1, 1)
         quantize_f(2)
-        group_w(1, 1)
-        quantize_w(1, 0)
-        group_w(1, 2)
         dw_store(1)
-        quantize_w(1, 1)
         step(4)
-        quantize_w(1, 2)
         group_m(0, 0, VC)
         quantize_f(3)
         quantize_m(0, 0)
@@ -535,24 +550,26 @@ def tile_layer_simple_pa_v_kernel(
         dw_store(3)
         step(6, words=(VC, VC))
         quantize_f(5)
-        for c in range(PACK):
+        dw_store(4)
+        for c in range(2):
             dx_tile(0, c)
-            if c == 0:
-                dw_store(4)
             dx_store(0, c, VC)
-        step(7, first=(S, VC, S), words=(VC, S))
-        quantize_f(6)
+        step(7, first=(S, VC, S), words=(S, S))
         group_m(1, 0, VC)
+        quantize_f(6)
         dw_store(5)
         step(8)
         quantize_m(1, 0)
         quantize_f(7)
         group_m(1, 1, VC)
         dw_store(6)
-        quantize_m(1, 1)
         step(9)
-        group_m(1, 2, VC, S)
-        dw_store(7)
+        dw_store(7, S)
+        quantize_m(1, 1)
+        for c in range(2, 4):
+            dx_tile(0, c)
+            dx_store(0, c, S)
+        group_m(1, 2, VC)
         dx_product(1, 0)
         dx_product(1, 1)
         quantize_m(1, 2)

@@ -19,7 +19,7 @@ P = 128
 PACK = 4
 G = 2
 SLOTS = G * PACK
-STAGES = 4
+STAGES = 7
 
 
 def tile_layer_simple_pa_v_kernel(
@@ -37,7 +37,7 @@ def tile_layer_simple_pa_v_kernel(
         def psum(name, shape, dtype, bank):
             return ps.tile([P] + shape, dtype, name=name, tag="bank%d" % bank)
 
-        turn = {"bank": 0, "stage": 0, "first": 3}
+        turn = {"bank": 0, "stage": 0, "first": 2}
 
         def next_bank(name, shape, dtype):
             bank = turn["first"] + turn["bank"] % (8 - turn["first"])
@@ -79,9 +79,11 @@ def tile_layer_simple_pa_v_kernel(
         wc_hbm = [w.rearrange("(p s) f -> p s f", s=PACK) for w in (cv2_w, cv1_w)]
         z_sb, g_sb, wc_raw, w_raw, x_raw = {}, {}, {}, {}, {}
 
+        z_pass = [sbuf("z%d" % g, [PACK, BS, N], F32) for g in range(G)]
+
         def load_z(k):
-            z_sb[k] = sbuf("z%d" % k, [BS, N], F32)
-            nc.sync.dma_start(out=z_sb[k][:], in_=z_hbm[k // PACK, k % PACK])
+            z_sb[k] = z_pass[k // PACK][:, k % PACK, :, :]
+            nc.sync.dma_start(out=z_sb[k], in_=z_hbm[k // PACK, k % PACK])
 
         def load_g(k):
             pair = sbuf("g%d" % k, [BS, 2, N], BF16)
@@ -149,7 +151,7 @@ def tile_layer_simple_pa_v_kernel(
 
         sum_zm = sbuf("sum_zm", [SLOTS], F32)
         sum_gzm = sbuf("sum_gzm", [SLOTS], F32)
-        sum_gm = [psum("sum_gm%d" % g, [PACK], F32, 1 + g) for g in range(G)]
+        sum_gm = psum("sum_gm", [SLOTS], F32, 1)
         gate = [sbuf("gate%d" % g, [BS, PACK, N], BF16) for g in range(G)]
         unread = sbuf("unread", [BS, N], F32, "dx_b0_j2")
         zm, g_t = {}, {}
@@ -158,7 +160,7 @@ def tile_layer_simple_pa_v_kernel(
             zm[k] = sbuf("zm%d" % k, [BS, N], F32, "zm%d" % (k % 3))
             nc.vector.scalar_tensor_tensor(
                 out=zm[k][:].rearrange("p b m -> p (b m)"),
-                in0=z_sb[k][:].rearrange("p b m -> p (b m)"),
+                in0=z_sb[k].rearrange("p b m -> p (b m)"),
                 scalar=0.0,
                 in1=mask_row_ps,
                 op0=ALU.max,
@@ -183,11 +185,10 @@ def tile_layer_simple_pa_v_kernel(
             nc.scalar.copy(out=g_t[k][:].rearrange("p k c e -> p (k c e)").bitcast(F32), in_=turned[:].rearrange("p k c -> p (k c)"))
 
         def sum_g(k):
-            g, s = divmod(k, PACK)
             for step in range(8):
                 blk, e = divmod(step, 2)
                 nc.tensor.matmul(
-                    sum_gm[g][:, s : s + 1], lhsT=g_t[k][:, blk, :, e], rhs=mask_col[:, blk, e : e + 1], start=(step == 0), stop=(step == 7)
+                    sum_gm[:, k : k + 1], lhsT=g_t[k][:, blk, :, e], rhs=mask_col[:, blk, e : e + 1], start=(step == 0), stop=(step == 7)
                 )
 
         def small(name, width=SLOTS):
@@ -196,82 +197,59 @@ def tile_layer_simple_pa_v_kernel(
         gamma_f = gamma_sb[:].rearrange("p g s -> p (g s)")
         mean_f = mean_sb[:].rearrange("p g s -> p (g s)")
         rstd_f = rstd_sb[:].rearrange("p g s -> p (g s)")
-        total, inv_total, share = small("total", 1), small("inv_total", 1), small("share", 1)
-        coef_a, a_over_total, rstd_sq, neg_k, mean_rest = (small(n) for n in ("coef_a", "a_over_total", "rstd_sq", "neg_k", "mean_rest"))
-        q1, q2, q3, q4, q5, neg_b, coef_c = (small(n) for n in ("q1", "q2", "q3", "q4", "q5", "neg_b", "coef_c"))
+        total, inv_total = small("total", 1), small("inv_total", 1)
+        coef_a, a_over_total, neg_rstd_sq, neg_k = (small(n) for n in ("coef_a", "a_over_total", "neg_rstd_sq", "neg_k"))
+        q0, q1, q2, q3, q4, q5, neg_b, coef_c = (small(n) for n in ("q0", "q1", "q2", "q3", "q4", "q5", "neg_b", "coef_c"))
         V = nc.vector
 
         const_steps = [
             [
                 lambda: V.tensor_reduce(out=total[:], in_=count_sb[:], axis=mybir.AxisListType.X, op=ALU.add),
                 lambda: V.tensor_tensor(out=coef_a[:], in0=rstd_f, in1=gamma_f, op=ALU.mult),
-                lambda: V.tensor_tensor(out=rstd_sq[:], in0=rstd_f, in1=rstd_f, op=ALU.mult),
+                lambda: V.scalar_tensor_tensor(out=neg_rstd_sq[:], in0=rstd_f, scalar=-1.0, in1=rstd_f, op0=ALU.mult, op1=ALU.mult),
             ],
             [lambda: V.reciprocal(out=inv_total[:], in_=total[:])],
-            [
-                lambda: V.tensor_scalar(out=a_over_total[:], in0=coef_a[:], scalar1=inv_total[:], scalar2=None, op0=ALU.mult),
-                lambda: V.tensor_scalar(out=share[:], in0=mask_sum[:], scalar1=inv_total[:], scalar2=-1.0, op0=ALU.mult, op1=ALU.mult),
-            ],
-            [
-                lambda: V.scalar_tensor_tensor(out=neg_k[:], in0=rstd_sq[:], scalar=-1.0, in1=a_over_total[:], op0=ALU.mult, op1=ALU.mult),
-                lambda: V.scalar_tensor_tensor(out=mean_rest[:], in0=mean_f, scalar=share[:], in1=mean_f, op0=ALU.mult, op1=ALU.add),
-            ],
+            [lambda: V.tensor_scalar(out=a_over_total[:], in0=coef_a[:], scalar1=inv_total[:], scalar2=None, op0=ALU.mult)],
+            [lambda: V.tensor_tensor(out=neg_k[:], in0=neg_rstd_sq[:], in1=a_over_total[:], op=ALU.mult)],
         ]
 
-        def stat_steps(g):
-            c = slice(g * PACK, (g + 1) * PACK)
-            return [
-                [
-                    lambda: V.tensor_tensor(out=q1[:, c], in0=mean_f[:, c], in1=sum_gm[g][:], op=ALU.mult),
-                    lambda: V.tensor_tensor(out=q4[:, c], in0=a_over_total[:, c], in1=sum_gm[g][:], op=ALU.mult),
-                    lambda: V.scalar_tensor_tensor(
-                        out=q3[:, c], in0=sum_zm[:, c], scalar=inv_total[:], in1=mean_rest[:, c], op0=ALU.mult, op1=ALU.add
-                    ),
-                ],
-                [lambda: V.tensor_tensor(out=q2[:, c], in0=sum_gzm[:, c], in1=q1[:, c], op=ALU.subtract)],
-                [lambda: V.tensor_tensor(out=neg_b[:, c], in0=q2[:, c], in1=neg_k[:, c], op=ALU.mult)],
-                [lambda: V.tensor_tensor(out=q5[:, c], in0=neg_b[:, c], in1=q3[:, c], op=ALU.mult)],
-                [
-                    lambda: V.scalar_tensor_tensor(
-                        out=coef_c[:, c], in0=q5[:, c], scalar=-1.0, in1=q4[:, c], op0=ALU.mult, op1=ALU.subtract
-                    )
-                ],
-            ]
+        stat_steps = [
+            [lambda: V.scalar_tensor_tensor(out=q0[:], in0=mean_f, scalar=mask_sum[:], in1=sum_zm[:], op0=ALU.mult, op1=ALU.subtract)],
+            [
+                lambda: V.tensor_tensor(out=q1[:], in0=mean_f, in1=sum_gm[:], op=ALU.mult),
+                lambda: V.tensor_tensor(out=q4[:], in0=a_over_total[:], in1=sum_gm[:], op=ALU.mult),
+                lambda: V.scalar_tensor_tensor(out=q3[:], in0=q0[:], scalar=inv_total[:], in1=mean_f, op0=ALU.mult, op1=ALU.subtract),
+            ],
+            [lambda: V.tensor_tensor(out=q2[:], in0=sum_gzm[:], in1=q1[:], op=ALU.subtract)],
+            [lambda: V.tensor_tensor(out=neg_b[:], in0=q2[:], in1=neg_k[:], op=ALU.mult)],
+            [lambda: V.tensor_tensor(out=q5[:], in0=neg_b[:], in1=q3[:], op=ALU.mult)],
+            [lambda: V.tensor_tensor(out=coef_c[:], in0=q5[:], in1=q4[:], op=ALU.subtract)],
+        ]
 
         def run(steps):
             for step in steps:
                 step()
 
-        affine, dz_bf, dz_stage = {}, {}, {}
+        dz_stage = {}
         dz_mx = mx_pair("dz", [BS, G, N])
 
-        def affine_z(g, b):
-            affine[g, b] = sbuf("affine%d%d" % (g, b), [PACK, N], F32, "affine%d" % g)
-            for s in range(PACK):
-                k = g * PACK + s
-                nc.scalar.activation(
-                    out=affine[g, b][:, s, :], in_=z_sb[k][:, b, :], func=ACT.Identity, scale=neg_b[:, k : k + 1], bias=coef_c[:, k : k + 1]
-                )
+        def affine_z(k, b):
+            nc.scalar.activation(out=z_sb[k][:, b, :], in_=z_sb[k][:, b, :], func=ACT.Identity, scale=neg_b[:, k : k + 1], bias=coef_c[:, k : k + 1])
 
         def weigh_gate(g, b):
             row = mask_row[:, b * N : (b + 1) * N].unsqueeze(1).to_broadcast([P, PACK, N])
             V.tensor_tensor(out=gate[g][:, b, :, :], in0=gate[g][:, b, :, :], in1=row, op=ALU.mult)
 
-        def add_g(g, b, s):
-            k = g * PACK + s
-            V.scalar_tensor_tensor(
-                out=affine[g, b][:, s, :], in0=g_sb[k][:, b, :], scalar=coef_a[:, k : k + 1], in1=affine[g, b][:, s, :], op0=ALU.mult, op1=ALU.add
-            )
+        def add_g(k, b):
+            V.scalar_tensor_tensor(out=z_sb[k][:, b, :], in0=g_sb[k][:, b, :], scalar=coef_a[:, k : k + 1], in1=z_sb[k][:, b, :], op0=ALU.mult, op1=ALU.add)
 
         def round_dz(g, b):
-            dz_bf[g, b] = sbuf("dz_bf%d%d" % (g, b), [PACK, N], BF16, "dz_bf%d" % g)
-            V.tensor_tensor(out=dz_bf[g, b][:], in0=affine[g, b][:], in1=gate[g][:, b, :, :], op=ALU.mult)
-
-        def group_dz(g, b):
             dz_stage[g, b] = next_stage("dz_stage%d%d" % (g, b), PACK * N)
-            V.tensor_copy(
-                out=dz_stage[g, b][:].rearrange("p (t x i s) -> p x t i s", t=PACK, i=2, s=PACK),
-                in_=dz_bf[g, b][:].rearrange("p s (x i t) -> p x t i s", i=2, t=PACK),
+            V.tensor_tensor(
+                out=dz_stage[g, b][:].rearrange("p (t x s) -> p x s t", t=PACK, s=PACK),
+                in0=z_pass[g][:, :, b, :].rearrange("p s (x t) -> p x s t", t=PACK),
+                in1=gate[g][:, b, :, :].rearrange("p s (x t) -> p x s t", t=PACK),
+                op=ALU.mult,
             )
 
         def quantize_dz(g, b):
@@ -341,7 +319,7 @@ def tile_layer_simple_pa_v_kernel(
         def round_dx(i, j, eng):
             b, t = divmod(i, PACK)
             if t == 0:
-                dx_bf[b, j] = sbuf("dx_bf%d%d" % (b, j), [PACK, NF], BF16, "dx_b0_j%d" % j if b == 0 else "z%d" % j)
+                dx_bf[b, j] = sbuf("dx_bf%d%d" % (b, j), [PACK, NF], BF16, "dx_b%d_j%d" % (b, j))
             out = dx_bf[b, j][:, t, :].rearrange("p (u w e) -> p u w e", u=2, e=2)
             eng(out=out, in_=dx_ps[i, j][:].rearrange("p (w u e) -> p u w e", u=2, e=2))
 
@@ -381,108 +359,96 @@ def tile_layer_simple_pa_v_kernel(
             )
             nc.sync.dma_start(out=dw_hbm[i // PACK, i % PACK], in_=dw_sb[i][:, 1, :])
 
-        def group_m(b, j, *engines):
-            key = "m%d%d" % (b, j)
-            staged[key] = next_stage("st_" + key, PACK * NF)
-            for u in range(2):
-                engines[u % len(engines)](
-                    out=staged[key][:, u * 1024 : (u + 1) * 1024].rearrange("p (e y i t) -> p y e i t", e=2, i=4, t=PACK),
-                    in_=dx_bf[b, j][:, :, u * 256 : (u + 1) * 256].rearrange("p t (y i e) -> p y e i t", i=4, e=2),
-                )
+        def group_m(b, j, u, eng):
+            key = "m%d%d%d" % (b, j, u)
+            staged[key] = next_stage("st_" + key, 2 * NF)
+            eng(
+                out=staged[key][:].rearrange("p (e y i t) -> p y e i t", e=2, i=4, t=PACK),
+                in_=dx_bf[b, j][:, :, u * 256 : (u + 1) * 256].rearrange("p t (y i e) -> p y e i t", i=4, e=2),
+            )
 
-        def quantize_m(b, j):
-            if j == 0:
+        def quantize_m(b, j, u):
+            if (j, u) == (0, 0):
                 m_mx[b] = mx_pair("m%d" % b, [J, NF], "m" if b == 0 else "wc")
-            quantize(m_mx[b], (every, j, every), staged["m%d%d" % (b, j)][:], E5M2)
+            quantize(m_mx[b], (every, j, slice(u * 256, (u + 1) * 256)), staged["m%d%d%d" % (b, j, u)][:], E5M2)
 
         dxo_ps = {}
 
-        def dx_product(b, j):
-            for c in range(PACK):
-                if j == 0:
-                    dxo_ps[b, c] = next_bank("dxo_ps%d%d" % (b, c), [N], F32)
-                mx_pass(dxo_ps[b, c][:], m_mx[b], (every, j, slice(c * P, (c + 1) * P)), E5M2, w_mx, (every, b, j, every), E4M3, j == 0, j == J - 1)
-
-        def dx_tile(b, c):
-            dxo_ps[b, c] = next_bank("dxo_ps%d%d" % (b, c), [N], F32)
+        def dx_tiles(b, u):
             for j in range(J):
-                mx_pass(dxo_ps[b, c][:], m_mx[b], (every, j, slice(c * P, (c + 1) * P)), E5M2, w_mx, (every, b, j, every), E4M3, j == 0, j == J - 1)
+                for c in (2 * u, 2 * u + 1):
+                    if j == 0:
+                        dxo_ps[b, c] = next_bank("dxo_ps%d%d" % (b, c), [N], F32)
+                    mx_pass(dxo_ps[b, c][:], m_mx[b], (every, j, slice(c * P, (c + 1) * P)), E5M2, w_mx, (every, b, j, every), E4M3, j == 0, j == J - 1)
 
         def dx_store(b, c, eng):
-            res = sbuf("dxo%d%d" % (b, c), [N], F32, ("zm0", "zm1", "zm2", "z3", "z4", "z5", "z6", "z7")[b * PACK + c])
+            res = sbuf("dxo%d%d" % (b, c), [N], F32, ("zm0", "zm1", "zm2", "g_t0", "g_t1", "gate0", "gate1", "g0")[b * PACK + c])
             eng(out=res[:], in_=dxo_ps[b, c][:])
             nc.sync.dma_start(out=dxo_hbm[b, c], in_=res[:])
 
         S = nc.scalar.copy
         VC = nc.vector.tensor_copy
 
-        stats0, stats1 = stat_steps(0), stat_steps(1)
-        after_relu = {4: const_steps[0], 5: const_steps[2], 6: stats0[0], 7: stats0[2]}
-        after_dot = {4: const_steps[1], 5: const_steps[3], 6: stats0[1], 7: stats0[3]}
+        after_relu = {4: const_steps[0], 5: const_steps[2], 7: stat_steps[0]}
+        after_dot = {4: const_steps[1], 5: const_steps[3]}
         relu_mask(0)
         spread_mask()
         sign_of(0)
         transpose_g(0)
         for k in range(1, SLOTS):
             relu_mask(k)
+            if k < SLOTS - 1:
+                transpose_g(k)
             sign_of(k)
-            transpose_g(k)
             sum_g(k - 1)
-            run(after_relu.get(k, []))
+            if k == SLOTS - 2:
+                transpose_g(k + 1)
             if k in (4, 6):
                 group_wc(0, k // 6)
+            run(after_relu.get(k, []))
             dot_g(k - 1)
             run(after_dot.get(k, []))
             if k == 6:
                 quantize_wc(0, 0)
         sum_g(SLOTS - 1)
-        quantize_wc(0, 1)
-        run(stats0[4])
-        affine_z(0, 0)
+        group_wc(0, 2)
+        run(stat_steps[1])
         dot_g(SLOTS - 1)
-        weigh_gate(0, 0)
-        run(stats1[0])
-        turn["first"], turn["bank"] = 0, 3
+        turn["first"], turn["bank"] = 0, 2
         group_wc(1, 2)
         group_x(0)
         group_w(0, 0)
         group_w(0, 1)
-        group_wc(0, 2)
-        add_g(0, 0, 0)
-        run(stats1[1])
-        add_g(0, 0, 1)
-        run(stats1[2])
-        add_g(0, 0, 2)
-        run(stats1[3])
-        add_g(0, 0, 3)
-        run(stats1[4])
-        affine_z(1, 0)
-        weigh_gate(1, 0)
-        group_wc(1, 0)
+        quantize_wc(0, 1)
         load_w(1)
-        round_dz(0, 0)
+        run(stat_steps[2])
+        weigh_gate(0, 0)
+        run(stat_steps[3])
+        group_wc(1, 0)
+        weigh_gate(1, 0)
+        run(stat_steps[4])
         quantize_wc(0, 2)
-        group_dz(0, 0)
-        group_wc(1, 1)
-        for s in range(PACK):
-            add_g(1, 0, s)
-        quantize_dz(0, 0)
+        run(stat_steps[5])
+        weigh_gate(0, 1)
         quantize_wc(1, 0)
-        fetch_grouped("wc12")
-        group_w(0, 2)
-        round_dz(1, 0)
-        quantize_wc(1, 1)
-        affine_z(0, 1)
-        group_dz(1, 0)
-        quantize_wc(1, 2)
+        for k in range(SLOTS):
+            affine_z(k, 0)
+            add_g(k, 0)
+            if k == 3:
+                fetch_grouped("wc12")
+                group_w(0, 2)
+                round_dz(0, 0)
+        group_wc(1, 1)
+        quantize_dz(0, 0)
         fetch_grouped("x0")
         group_x(1)
+        round_dz(1, 0)
         fetch_grouped("w00")
         group_w(1, 0)
-        quantize_dz(1, 0)
+        quantize_wc(1, 2)
+        quantize_wc(1, 1)
         fetch_grouped("w01")
-        quantize_x(0)
-        quantize_w(0, 0)
+        quantize_dz(1, 0)
         fetch_grouped("w02")
 
         def step(i, first=(S, S, S), words=(S, S), second=(S, S, S)):
@@ -502,77 +468,93 @@ def tile_layer_simple_pa_v_kernel(
                 for j in range(J):
                     dw_out(i - 2, j, second[j])
 
-        step(0)
-        weigh_gate(0, 1)
-        fetch_grouped("x1")
-        quantize_w(0, 1)
-        fetch_grouped("w10")
-        group_w(1, 1)
-        for s in range(PACK):
-            add_g(0, 1, s)
-        affine_z(1, 1)
-        quantize_w(0, 2)
+        first_product(0)
+        quantize_x(0)
+        quantize_w(0, 0)
         weigh_gate(1, 1)
+        quantize_w(0, 1)
+        for k in range(PACK):
+            affine_z(k, 1)
+            add_g(k, 1)
+        for j in range(J):
+            round_dx(0, j, S)
+        quantize_w(0, 2)
+        round_dz(0, 1)
+        fetch_grouped("x1")
+        group_w(1, 1)
+        for k in range(PACK, SLOTS):
+            affine_z(k, 1)
+            add_g(k, 1)
+        fetch_grouped("w10")
+        quantize_dz(0, 1)
         step(1)
+        round_dz(1, 1)
         quantize_x(1)
+        quantize_f(0)
+        quantize_w(1, 0)
+        quantize_dz(1, 1)
         fetch_grouped("w11")
         group_w(1, 2)
-        round_dz(0, 1)
-        quantize_w(1, 0)
-        fetch_grouped("w12")
-        group_dz(0, 1)
-        quantize_f(0)
-        step(2)
         quantize_w(1, 1)
-        for s in range(PACK):
-            add_g(1, 1, s)
-        quantize_dz(0, 1)
-        quantize_f(1)
-        round_dz(1, 1)
+        fetch_grouped("w12")
+        step(2, words=(VC, VC))
         quantize_w(1, 2)
-        step(3)
-        group_dz(1, 1)
+        quantize_f(1)
         dw_store(0)
-        quantize_dz(1, 1)
+        step(3, words=(VC, VC))
         quantize_f(2)
         dw_store(1)
-        step(4)
-        group_m(0, 0, VC)
-        quantize_f(3)
-        quantize_m(0, 0)
-        group_m(0, 1, VC)
-        dw_store(2)
-        quantize_m(0, 1)
-        step(5)
-        group_m(0, 2, VC)
-        quantize_f(4)
-        quantize_m(0, 2)
-        dw_store(3)
+        for i in (4, 5):
+            step(i)
+            u = i - 4
+            group_m(0, 0, u, VC)
+            group_m(0, 1, u, VC)
+            quantize_f(i - 1)
+            quantize_m(0, 0, u)
+            group_m(0, 2, u, VC)
+            quantize_m(0, 1, u)
+            dw_store(i - 2)
+            quantize_m(0, 2, u)
+            if u == 1:
+                dx_tiles(0, 0)
+                dx_store(0, 0, S)
+                dx_store(0, 1, VC)
         step(6, words=(VC, VC))
         quantize_f(5)
+        dx_tiles(0, 1)
+        dx_store(0, 2, VC)
+        dx_store(0, 3, VC)
         dw_store(4)
-        for c in range(2):
-            dx_tile(0, c)
-            dx_store(0, c, VC)
         step(7, first=(S, VC, S), words=(S, S))
-        group_m(1, 0, VC)
+        turn_words(7)
+        group_m(1, 0, 0, VC)
         quantize_f(6)
-        dw_store(5)
-        step(8)
-        quantize_m(1, 0)
+        dw_product(6)
+        group_words(7, 0, VC)
+        group_words(7, 1, VC)
+        group_m(1, 1, 0, VC)
         quantize_f(7)
-        group_m(1, 1, VC)
+        dw_product(7)
+        dw_store(5)
+        for j in range(J):
+            dw_out(6, j, S)
+        quantize_m(1, 0, 0)
+        group_m(1, 2, 0, VC)
+        quantize_m(1, 1, 0)
         dw_store(6)
-        step(9)
-        dw_store(7, S)
-        quantize_m(1, 1)
-        for c in range(2, 4):
-            dx_tile(0, c)
-            dx_store(0, c, S)
-        group_m(1, 2, VC)
-        dx_product(1, 0)
-        dx_product(1, 1)
-        quantize_m(1, 2)
-        dx_product(1, 2)
-        for c in range(PACK):
-            dx_store(1, c, VC if c % 2 else S)
+        quantize_m(1, 2, 0)
+        for j in range(J):
+            dw_out(7, j, S)
+        dx_tiles(1, 0)
+        group_m(1, 1, 1, S)
+        group_m(1, 0, 1, VC)
+        dw_store(7)
+        group_m(1, 2, 1, S)
+        quantize_m(1, 0, 1)
+        quantize_m(1, 1, 1)
+        dx_store(1, 0, VC)
+        quantize_m(1, 2, 1)
+        dx_store(1, 1, S)
+        dx_tiles(1, 1)
+        dx_store(1, 2, S)
+        dx_store(1, 3, VC)

@@ -17,15 +17,26 @@ ACT = mybir.ActivationFunctionType
 
 P = 128
 PACK = 4
-G = 2
-SLOTS = G * PACK
+CONVS = 2
+SLOTS = CONVS * PACK
+UNITS = BS * PACK
+BANKS = 8
+HELD_BANKS = 2
 STAGES = 7
+RELU_BUFS = 3
+BIG_BUFS = 3
+HALF = NF // 2
 
 
 def tile_layer_simple_pa_v_kernel(
     tc, X, W, N_batch, mask, cv1_w, cv1_b, cv2_w, cv2_b, bn_gamma, bn_beta, z, mean, rstd, grad_out, out_0, out_1
 ):
     nc = tc.nc
+    vec = nc.vector
+    on_scalar = nc.scalar.copy
+    on_vector = nc.vector.tensor_copy
+    every = slice(None)
+
     with ExitStack() as ctx:
         sb = ctx.enter_context(tc.tile_pool(name="sb", bufs=1))
         ps = ctx.enter_context(tc.psum_pool(name="ps", bufs=1))
@@ -37,10 +48,10 @@ def tile_layer_simple_pa_v_kernel(
         def psum(name, shape, dtype, bank):
             return ps.tile([P] + shape, dtype, name=name, tag="bank%d" % bank)
 
-        turn = {"bank": 0, "stage": 0, "first": 2}
+        turn = {"bank": 0, "first_bank": HELD_BANKS, "stage": 0}
 
         def next_bank(name, shape, dtype):
-            bank = turn["first"] + turn["bank"] % (8 - turn["first"])
+            bank = turn["first_bank"] + turn["bank"] % (BANKS - turn["first_bank"])
             turn["bank"] = turn["bank"] + 1
             return psum(name, shape, dtype, bank)
 
@@ -54,38 +65,39 @@ def tile_layer_simple_pa_v_kernel(
             return sbuf(name + "_codes", shape, U32, place + "_c"), sbuf(name + "_scales", shape, U8, place + "_s")
 
         def quantize(pair, where, src, fmt):
-            nc.vector.quantize_mx(out=pair[0][where].bitcast(fmt), scales=pair[1][where], in_=src)
+            vec.quantize_mx(out=pair[0][where].bitcast(fmt), scales=pair[1][where], in_=src)
 
-        def mx_pass(out, left, left_at, left_fmt, right, right_at, right_fmt, start, stop):
+        def mx_pass(out, grad, grad_at, other, other_at, start, stop):
             nc.tensor.matmul_mx(
                 out=out,
-                lhsT=left[0][left_at].bitcast(left_fmt),
-                lhsT_scale=left[1][left_at],
-                rhs=right[0][right_at].bitcast(right_fmt),
-                rhs_scale=right[1][right_at],
+                lhsT=grad[0][grad_at].bitcast(E5M2),
+                lhsT_scale=grad[1][grad_at],
+                rhs=other[0][other_at].bitcast(E4M3),
+                rhs_scale=other[1][other_at],
                 start=start,
                 stop=stop,
             )
 
-        every = slice(None)
+        def run(calls):
+            for call in calls:
+                call()
 
         ident_f32 = sbuf("ident_f32", [P], F32)
         make_identity(nc, ident_f32[:])
         ident_bf = sbuf("ident_bf", [P], BF16)
         make_identity(nc, ident_bf[:])
 
-        z_hbm = z.rearrange("b (g p s) m -> g s p b m", g=G, s=PACK)
-        g_hbm = grad_out.rearrange("b (g p h s) m -> g h p b s m", g=G, h=2, s=2)
+        z_hbm = z.rearrange("b (g p s) m -> g s p b m", g=CONVS, s=PACK)
+        g_hbm = grad_out.rearrange("b (g p h s) m -> g h p b s m", g=CONVS, h=2, s=2)
         wc_hbm = [w.rearrange("(p s) f -> p s f", s=PACK) for w in (cv2_w, cv1_w)]
+        z_conv = [sbuf("z%d" % g, [PACK, BS, N], F32) for g in range(CONVS)]
         z_sb, g_sb, wc_raw, w_raw, x_raw = {}, {}, {}, {}, {}
 
-        z_pass = [sbuf("z%d" % g, [PACK, BS, N], F32) for g in range(G)]
-
         def load_z(k):
-            z_sb[k] = z_pass[k // PACK][:, k % PACK, :, :]
+            z_sb[k] = z_conv[k // PACK][:, k % PACK, :, :]
             nc.sync.dma_start(out=z_sb[k], in_=z_hbm[k // PACK, k % PACK])
 
-        def load_g(k):
+        def load_g_pair(k):
             pair = sbuf("g%d" % k, [BS, 2, N], BF16)
             nc.sync.dma_start(out=pair[:], in_=g_hbm[k // PACK, (k % PACK) // 2])
             g_sb[k], g_sb[k + 1] = pair[:, :, 0, :], pair[:, :, 1, :]
@@ -100,228 +112,207 @@ def tile_layer_simple_pa_v_kernel(
             x_raw[b] = sbuf("x_raw%d" % b, [PACK, N], BF16)
             nc.sync.dma_start(out=x_raw[b][:], in_=X[b].rearrange("(p t) n -> p t n", t=PACK))
 
-        def load_w(b):
-            w_raw[b] = sbuf("w_raw%d" % b, [PACK, N * J], BF16, "big%d" % (2 if b == 0 else 0))
+        def load_w(b, place):
+            w_raw[b] = sbuf("w_raw%d" % b, [PACK, N * J], BF16, place)
             nc.sync.dma_start(out=w_raw[b][:], in_=W[b].rearrange("(p t) n j -> p t (n j)", t=PACK))
 
-        mask_col = sbuf("mask_col", [4, 2], BF16)
+        mask_col = sbuf("mask_col", [2 * BS, 2], BF16)
         nc.sync.dma_start(out=mask_col[:], in_=mask.rearrange("b o (h w e) -> w (b o h) e", h=2, e=2))
         load_z(0)
-        load_z(1)
-        load_g(0)
-        load_z(2)
-        load_g(2)
-        load_z(3)
-        load_wc(0, 0)
-        gamma_sb = sbuf("gamma_sb", [G, PACK], BF16)
-        mean_sb = sbuf("mean_sb", [G, PACK], F32)
-        rstd_sb = sbuf("rstd_sb", [G, PACK], F32)
+        gamma_sb = sbuf("gamma_sb", [CONVS, PACK], BF16)
+        mean_sb = sbuf("mean_sb", [CONVS, PACK], F32)
+        rstd_sb = sbuf("rstd_sb", [CONVS, PACK], F32)
         count_sb = sbuf("count_sb", [BS], BF16)
-        nc.sync.dma_start(out=count_sb[:], in_=N_batch.partition_broadcast(P))
-        for tile, vec in ((gamma_sb, bn_gamma), (mean_sb, mean), (rstd_sb, rstd)):
-            nc.sync.dma_start(out=tile[:], in_=vec.rearrange("(g p s) -> p g s", g=G, s=PACK))
-        load_z(4)
-        load_g(4)
-        load_z(5)
-        load_wc(0, 1)
-        load_z(6)
-        load_g(6)
-        load_z(7)
-        load_wc(0, 2)
+        nc.scalar.dma_start(out=count_sb[:], in_=N_batch.partition_broadcast(P))
+        for tile, vector in ((rstd_sb, rstd), (gamma_sb, bn_gamma), (mean_sb, mean)):
+            nc.scalar.dma_start(out=tile[:], in_=vector.rearrange("(g p s) -> p g s", g=CONVS, s=PACK))
+        load_z(1)
+        load_g_pair(0)
+        for pair in range(1, SLOTS // 2):
+            load_z(2 * pair)
+            load_g_pair(2 * pair)
+            load_z(2 * pair + 1)
+            load_wc(0, pair - 1)
         for j in range(J):
             load_wc(1, j)
         load_x(0)
-        load_w(0)
+        load_w(0, "big2")
         load_x(1)
 
-        def mask_in_psum(tile):
+        def mask_row_in(tile):
             words = mask_col[:].rearrange("p k e -> p (k e)").bitcast(F32)
-            for blk in range(4):
+            for blk in range(2 * BS):
                 nc.tensor.transpose(tile[:, blk, :], words[:, blk : blk + 1].to_broadcast([P, P]), ident_f32[:])
             return tile[:].rearrange("p k w -> p (k w)").bitcast(BF16)
 
-        mask_row_ps = mask_in_psum(psum("mask_ps", [4, P], F32, 0))
+        mask_row_ps = mask_row_in(psum("mask_ps", [2 * BS, P], F32, 0))
         mask_row = sbuf("mask_row", [BS * N], BF16)
-        mask_sum = sbuf("mask_sum", [1], F32)
+        s0 = sbuf("s0", [1], F32)
 
-        def spread_mask():
-            nc.scalar.activation(
-                out=mask_row[:], in_=mask_in_psum(next_bank("mask_ps2", [4, P], F32)), func=ACT.Identity, accum_out=mask_sum[:]
-            )
+        def copy_mask_row():
+            row = mask_row_in(next_bank("mask_ps2", [2 * BS, P], F32))
+            nc.scalar.activation(out=mask_row[:], in_=row, func=ACT.Identity, accum_out=s0[:])
 
-        sum_zm = sbuf("sum_zm", [SLOTS], F32)
-        sum_gzm = sbuf("sum_gzm", [SLOTS], F32)
-        sum_gm = psum("sum_gm", [SLOTS], F32, 1)
-        gate = [sbuf("gate%d" % g, [BS, PACK, N], BF16) for g in range(G)]
-        unread = sbuf("unread", [BS, N], F32, "dx_b0_j2")
-        zm, g_t = {}, {}
+        s3 = sbuf("s3", [SLOTS], F32)
+        s2 = sbuf("s2", [SLOTS], F32)
+        s1 = psum("s1", [SLOTS], F32, 1)
+        gate = [sbuf("gate%d" % g, [BS, PACK, N], BF16) for g in range(CONVS)]
+        s2_terms = sbuf("s2_terms", [BS, N], F32, "dx_b0_j2")
+        relu_m, g_turned = {}, {}
 
-        def relu_mask(k):
-            zm[k] = sbuf("zm%d" % k, [BS, N], F32, "zm%d" % (k % 3))
-            nc.vector.scalar_tensor_tensor(
-                out=zm[k][:].rearrange("p b m -> p (b m)"),
+        def relu_times_mask(k):
+            relu_m[k] = sbuf("relu_m%d" % k, [BS, N], F32, "relu%d" % (k % RELU_BUFS))
+            vec.scalar_tensor_tensor(
+                out=relu_m[k][:].rearrange("p b m -> p (b m)"),
                 in0=z_sb[k].rearrange("p b m -> p (b m)"),
                 scalar=0.0,
                 in1=mask_row_ps,
                 op0=ALU.max,
                 op1=ALU.mult,
-                accum_out=sum_zm[:, k : k + 1],
+                accum_out=s3[:, k : k + 1],
             )
 
-        def sign_of(k):
-            nc.scalar.activation(out=gate[k // PACK][:, :, k % PACK, :], in_=zm[k][:], func=ACT.Sign)
+        def open_gate(k):
+            nc.scalar.activation(out=gate[k // PACK][:, :, k % PACK, :], in_=relu_m[k][:], func=ACT.Sign)
 
-        def dot_g(k):
-            nc.vector.scalar_tensor_tensor(
-                out=unread[:], in0=zm[k][:], scalar=1.0, in1=g_sb[k], op0=ALU.mult, op1=ALU.mult, accum_out=sum_gzm[:, k : k + 1]
+        def sum_s2(k):
+            vec.scalar_tensor_tensor(
+                out=s2_terms[:], in0=relu_m[k][:], scalar=1.0, in1=g_sb[k], op0=ALU.mult, op1=ALU.mult, accum_out=s2[:, k : k + 1]
             )
 
-        def transpose_g(k):
-            turned = next_bank("g_turned%d" % k, [4, P], F32)
-            for blk in range(4):
+        def turn_g(k):
+            bank = next_bank("g_ps%d" % k, [2 * BS, P], F32)
+            for blk in range(2 * BS):
                 b, h = divmod(blk, 2)
-                nc.tensor.transpose(turned[:, blk, :], g_sb[k][:, b, :].bitcast(F32)[:, h * P : (h + 1) * P], ident_f32[:])
-            g_t[k] = sbuf("g_t%d" % k, [4, P, 2], BF16, "g_t%d" % (k % 2))
-            nc.scalar.copy(out=g_t[k][:].rearrange("p k c e -> p (k c e)").bitcast(F32), in_=turned[:].rearrange("p k c -> p (k c)"))
+                nc.tensor.transpose(bank[:, blk, :], g_sb[k][:, b, :].bitcast(F32)[:, h * P : (h + 1) * P], ident_f32[:])
+            g_turned[k] = sbuf("g_turned%d" % k, [2 * BS, P, 2], BF16, "g_turned%d" % (k % 2))
+            on_scalar(out=g_turned[k][:].rearrange("p k c e -> p (k c e)").bitcast(F32), in_=bank[:].rearrange("p k c -> p (k c)"))
 
-        def sum_g(k):
-            for step in range(8):
-                blk, e = divmod(step, 2)
+        def sum_s1(k):
+            last = 4 * BS - 1
+            for term in range(last + 1):
+                blk, e = divmod(term, 2)
                 nc.tensor.matmul(
-                    sum_gm[:, k : k + 1], lhsT=g_t[k][:, blk, :, e], rhs=mask_col[:, blk, e : e + 1], start=(step == 0), stop=(step == 7)
+                    s1[:, k : k + 1], lhsT=g_turned[k][:, blk, :, e], rhs=mask_col[:, blk, e : e + 1], start=(term == 0), stop=(term == last)
                 )
 
-        def small(name, width=SLOTS):
-            return sbuf(name, [width], F32)
-
-        gamma_f = gamma_sb[:].rearrange("p g s -> p (g s)")
-        mean_f = mean_sb[:].rearrange("p g s -> p (g s)")
-        rstd_f = rstd_sb[:].rearrange("p g s -> p (g s)")
-        total, inv_total = small("total", 1), small("inv_total", 1)
-        coef_a, a_over_total, neg_rstd_sq, neg_k = (small(n) for n in ("coef_a", "a_over_total", "neg_rstd_sq", "neg_k"))
-        q0, q1, q2, q3, q4, q5, neg_b, coef_c = (small(n) for n in ("q0", "q1", "q2", "q3", "q4", "q5", "neg_b", "coef_c"))
-        V = nc.vector
-
-        const_steps = [
+        gamma_c = gamma_sb[:].rearrange("p g s -> p (g s)")
+        mean_c = mean_sb[:].rearrange("p g s -> p (g s)")
+        rstd_c = rstd_sb[:].rearrange("p g s -> p (g s)")
+        total, inv_total = sbuf("total", [1], F32), sbuf("inv_total", [1], F32)
+        coef_a, a_per_total, neg_rstd_sq, neg_b_factor = (
+            sbuf(name, [SLOTS], F32) for name in ("coef_a", "a_per_total", "neg_rstd_sq", "neg_b_factor")
+        )
+        neg_rest, mean_s1, centred_s2, neg_level, a_s1, b_level, neg_b, coef_c = (
+            sbuf(name, [SLOTS], F32) for name in ("neg_rest", "mean_s1", "centred_s2", "neg_level", "a_s1", "b_level", "neg_b", "coef_c")
+        )
+        input_levels = [
             [
-                lambda: V.tensor_reduce(out=total[:], in_=count_sb[:], axis=mybir.AxisListType.X, op=ALU.add),
-                lambda: V.tensor_tensor(out=coef_a[:], in0=rstd_f, in1=gamma_f, op=ALU.mult),
-                lambda: V.scalar_tensor_tensor(out=neg_rstd_sq[:], in0=rstd_f, scalar=-1.0, in1=rstd_f, op0=ALU.mult, op1=ALU.mult),
+                lambda: vec.tensor_reduce(out=total[:], in_=count_sb[:], axis=mybir.AxisListType.X, op=ALU.add),
+                lambda: vec.tensor_tensor(out=coef_a[:], in0=rstd_c, in1=gamma_c, op=ALU.mult),
+                lambda: vec.scalar_tensor_tensor(out=neg_rstd_sq[:], in0=rstd_c, scalar=-1.0, in1=rstd_c, op0=ALU.mult, op1=ALU.mult),
             ],
-            [lambda: V.reciprocal(out=inv_total[:], in_=total[:])],
-            [lambda: V.tensor_scalar(out=a_over_total[:], in0=coef_a[:], scalar1=inv_total[:], scalar2=None, op0=ALU.mult)],
-            [lambda: V.tensor_tensor(out=neg_k[:], in0=neg_rstd_sq[:], in1=a_over_total[:], op=ALU.mult)],
+            [lambda: vec.reciprocal(out=inv_total[:], in_=total[:])],
+            [lambda: vec.tensor_scalar(out=a_per_total[:], in0=coef_a[:], scalar1=inv_total[:], scalar2=None, op0=ALU.mult)],
+            [lambda: vec.tensor_tensor(out=neg_b_factor[:], in0=neg_rstd_sq[:], in1=a_per_total[:], op=ALU.mult)],
+        ]
+        sum_levels = [
+            [lambda: vec.scalar_tensor_tensor(out=neg_rest[:], in0=mean_c, scalar=s0[:], in1=s3[:], op0=ALU.mult, op1=ALU.subtract)],
+            [
+                lambda: vec.tensor_tensor(out=mean_s1[:], in0=mean_c, in1=s1[:], op=ALU.mult),
+                lambda: vec.tensor_tensor(out=a_s1[:], in0=a_per_total[:], in1=s1[:], op=ALU.mult),
+                lambda: vec.scalar_tensor_tensor(
+                    out=neg_level[:], in0=neg_rest[:], scalar=inv_total[:], in1=mean_c, op0=ALU.mult, op1=ALU.subtract
+                ),
+            ],
+            [lambda: vec.tensor_tensor(out=centred_s2[:], in0=s2[:], in1=mean_s1[:], op=ALU.subtract)],
+            [lambda: vec.tensor_tensor(out=neg_b[:], in0=centred_s2[:], in1=neg_b_factor[:], op=ALU.mult)],
+            [lambda: vec.tensor_tensor(out=b_level[:], in0=neg_b[:], in1=neg_level[:], op=ALU.mult)],
+            [lambda: vec.tensor_tensor(out=coef_c[:], in0=b_level[:], in1=a_s1[:], op=ALU.subtract)],
         ]
 
-        stat_steps = [
-            [lambda: V.scalar_tensor_tensor(out=q0[:], in0=mean_f, scalar=mask_sum[:], in1=sum_zm[:], op0=ALU.mult, op1=ALU.subtract)],
-            [
-                lambda: V.tensor_tensor(out=q1[:], in0=mean_f, in1=sum_gm[:], op=ALU.mult),
-                lambda: V.tensor_tensor(out=q4[:], in0=a_over_total[:], in1=sum_gm[:], op=ALU.mult),
-                lambda: V.scalar_tensor_tensor(out=q3[:], in0=q0[:], scalar=inv_total[:], in1=mean_f, op0=ALU.mult, op1=ALU.subtract),
-            ],
-            [lambda: V.tensor_tensor(out=q2[:], in0=sum_gzm[:], in1=q1[:], op=ALU.subtract)],
-            [lambda: V.tensor_tensor(out=neg_b[:], in0=q2[:], in1=neg_k[:], op=ALU.mult)],
-            [lambda: V.tensor_tensor(out=q5[:], in0=neg_b[:], in1=q3[:], op=ALU.mult)],
-            [lambda: V.tensor_tensor(out=coef_c[:], in0=q5[:], in1=q4[:], op=ALU.subtract)],
-        ]
-
-        def run(steps):
-            for step in steps:
-                step()
-
-        dz_stage = {}
-        dz_mx = mx_pair("dz", [BS, G, N])
-
-        def affine_z(k, b):
-            nc.scalar.activation(out=z_sb[k][:, b, :], in_=z_sb[k][:, b, :], func=ACT.Identity, scale=neg_b[:, k : k + 1], bias=coef_c[:, k : k + 1])
+        staged = {}
+        dz_mx = mx_pair("dz", [BS, CONVS, N])
 
         def weigh_gate(g, b):
             row = mask_row[:, b * N : (b + 1) * N].unsqueeze(1).to_broadcast([P, PACK, N])
-            V.tensor_tensor(out=gate[g][:, b, :, :], in0=gate[g][:, b, :, :], in1=row, op=ALU.mult)
+            vec.tensor_tensor(out=gate[g][:, b, :, :], in0=gate[g][:, b, :, :], in1=row, op=ALU.mult)
 
-        def add_g(k, b):
-            V.scalar_tensor_tensor(out=z_sb[k][:, b, :], in0=g_sb[k][:, b, :], scalar=coef_a[:, k : k + 1], in1=z_sb[k][:, b, :], op0=ALU.mult, op1=ALU.add)
+        def ungated_dz(g, b):
+            for k in range(g * PACK, (g + 1) * PACK):
+                here, col = z_sb[k][:, b, :], slice(k, k + 1)
+                nc.scalar.activation(out=here, in_=here, func=ACT.Identity, scale=neg_b[:, col], bias=coef_c[:, col])
+                vec.scalar_tensor_tensor(out=here, in0=g_sb[k][:, b, :], scalar=coef_a[:, col], in1=here, op0=ALU.mult, op1=ALU.add)
 
         def round_dz(g, b):
-            dz_stage[g, b] = next_stage("dz_stage%d%d" % (g, b), PACK * N)
-            V.tensor_tensor(
-                out=dz_stage[g, b][:].rearrange("p (t x s) -> p x s t", t=PACK, s=PACK),
-                in0=z_pass[g][:, :, b, :].rearrange("p s (x t) -> p x s t", t=PACK),
+            staged["dz", g, b] = next_stage("dz_stage%d%d" % (g, b), PACK * N)
+            vec.tensor_tensor(
+                out=staged["dz", g, b][:].rearrange("p (t x s) -> p x s t", t=PACK, s=PACK),
+                in0=z_conv[g][:, :, b, :].rearrange("p s (x t) -> p x s t", t=PACK),
                 in1=gate[g][:, b, :, :].rearrange("p s (x t) -> p x s t", t=PACK),
                 op=ALU.mult,
             )
 
         def quantize_dz(g, b):
-            quantize(dz_mx, (every, b, g, every), dz_stage[g, b][:], E5M2)
+            quantize(dz_mx, (every, b, g, every), staged["dz", g, b][:], E5M2)
 
-        wc_mx = mx_pair("wc", [G, J, NF])
-        w_mx = mx_pair("w", [BS, J, N])
-        x_mx = mx_pair("x", [BS, N])
-        staged = {}
-
-        def group_on_scalar(key, src):
-            staged[key] = next_stage("st_" + key, PACK * N)
-            nc.scalar.copy(
-                out=staged[key][:].rearrange("p (c i t) -> p c t i", i=4, t=PACK), in_=src.rearrange("p t (c i) -> p c t i", i=4)
-            )
-
+        e4m3_mx = {"wc": mx_pair("wc", [CONVS, J, NF]), "w": mx_pair("w", [BS, J, N]), "x": mx_pair("x", [BS, N])}
         grouped_ps = {}
 
-        def group_on_tensor(key, src):
-            grouped_ps[key] = [next_bank("grp_%s_%d" % (key, half), [2, P, PACK], BF16) for half in range(2)]
-            for q in range(4):
+        def raw_rows(key):
+            if key[0] == "wc":
+                return wc_raw[key[1]][:, :, key[2] * NF : (key[2] + 1) * NF]
+            if key[0] == "x":
+                return x_raw[key[1]][:]
+            return w_raw[key[1]][:].rearrange("p t (n j) -> p j t n", j=J)[:, key[2], :, :]
+
+        def key_name(key):
+            return "_".join(str(part) for part in key)
+
+        def group_on_scalar(*key):
+            staged[key] = next_stage("st_" + key_name(key), PACK * N)
+            on_scalar(
+                out=staged[key][:].rearrange("p (c i t) -> p c t i", i=4, t=PACK), in_=raw_rows(key).rearrange("p t (c i) -> p c t i", i=4)
+            )
+
+        def group_on_tensor(*key):
+            grouped_ps[key] = [next_bank("grp_%s_%d" % (key_name(key), half), [2, P, PACK], BF16) for half in range(2)]
+            for q in range(N // P):
                 nc.tensor.matmul(
                     grouped_ps[key][q // 2][:, q % 2, :, :].rearrange("p (c i) t -> p c t i", i=8),
                     lhsT=ident_bf[:],
-                    rhs=src[:, :, q * P : (q + 1) * P].rearrange("p t (c i) -> p c t i", i=8),
+                    rhs=raw_rows(key)[:, :, q * P : (q + 1) * P].rearrange("p t (c i) -> p c t i", i=8),
                     start=True,
                     stop=True,
                 )
 
-        def fetch_grouped(key):
-            staged[key] = next_stage("st_" + key, PACK * N)
+        def fetch_grouped(*key):
+            staged[key] = next_stage("st_" + key_name(key), PACK * N)
             for half in range(2):
-                nc.scalar.copy(out=staged[key][:, half * 1024 : (half + 1) * 1024], in_=grouped_ps[key][half][:].rearrange("p q c t -> p (q c t)"))
+                cols = slice(half * 2 * N, (half + 1) * 2 * N)
+                on_scalar(out=staged[key][:, cols], in_=grouped_ps[key][half][:].rearrange("p q c t -> p (q c t)"))
 
-        def group_wc(g, j):
-            src = wc_raw[g][:, :, j * NF : (j + 1) * NF]
-            (group_on_tensor if (g, j) == (G - 1, J - 1) else group_on_scalar)("wc%d%d" % (g, j), src)
+        def quantize_e4m3(*key):
+            quantize(e4m3_mx[key[0]], (every,) + key[1:] + (every,), staged[key][:], E4M3)
 
-        def quantize_wc(g, j):
-            quantize(wc_mx, (every, g, j, every), staged["wc%d%d" % (g, j)][:], E4M3)
-
-        def group_x(b):
-            group_on_tensor("x%d" % b, x_raw[b][:])
-
-        def quantize_x(b):
-            quantize(x_mx, (every, b, every), staged["x%d" % b][:], E4M3)
-
-        def group_w(b, j):
-            group_on_tensor("w%d%d" % (b, j), w_raw[b][:].rearrange("p t (n j) -> p j t n", j=J)[:, j, :, :])
-
-        def quantize_w(b, j):
-            quantize(w_mx, (every, b, j, every), staged["w%d%d" % (b, j)][:], E4M3)
-
-        dx_bf, f_stage, f_mx, dw_sb, dx_ps, dw_ps, word_ps, m_mx = {}, {}, {}, {}, {}, {}, {}, {}
+        dx_ps, dx_bf, word_ps, f_mx, dw_ps, dw_sb = {}, {}, {}, {}, {}, {}
         dw_hbm = out_1.rearrange("b (p t) n j -> b t p (n j)", t=PACK)
-        dxo_hbm = out_0.rearrange("b (p c) n -> b c p n", c=PACK)
 
         def first_product(i):
             b, t = divmod(i, PACK)
             for j in range(J):
                 dx_ps[i, j] = next_bank("dx_ps%d%d" % (i, j), [NF], F32)
-                for g in range(G):
-                    mx_pass(
-                        dx_ps[i, j][:], dz_mx, (every, b, g, slice(t * P, (t + 1) * P)), E5M2, wc_mx, (every, g, j, every), E4M3, g == 0, g == G - 1
-                    )
+                for g in range(CONVS):
+                    nodes = (every, b, g, slice(t * P, (t + 1) * P))
+                    mx_pass(dx_ps[i, j][:], dz_mx, nodes, e4m3_mx["wc"], (every, g, j, every), g == 0, g == CONVS - 1)
 
-        def round_dx(i, j, eng):
+        def round_dx(i):
             b, t = divmod(i, PACK)
-            if t == 0:
-                dx_bf[b, j] = sbuf("dx_bf%d%d" % (b, j), [PACK, NF], BF16, "dx_b%d_j%d" % (b, j))
-            out = dx_bf[b, j][:, t, :].rearrange("p (u w e) -> p u w e", u=2, e=2)
-            eng(out=out, in_=dx_ps[i, j][:].rearrange("p (w u e) -> p u w e", u=2, e=2))
+            for j in range(J):
+                if t == 0:
+                    dx_bf[b, j] = sbuf("dx_bf%d%d" % (b, j), [PACK, NF], BF16, "dx_b%d_j%d" % (b, j))
+                out = dx_bf[b, j][:, t, :].rearrange("p (u w e) -> p u w e", u=2, e=2)
+                on_scalar(out=out, in_=dx_ps[i, j][:].rearrange("p (w u e) -> p u w e", u=2, e=2))
 
         def turn_words(i):
             b, t = divmod(i, PACK)
@@ -331,230 +322,226 @@ def tile_layer_simple_pa_v_kernel(
                 for u in range(2):
                     nc.tensor.transpose(word_ps[i][j // 2][:, j % 2, u, :], words[:, u * P : (u + 1) * P], ident_f32[:])
 
-        def group_words(i, part, eng):
-            if part == 0:
-                f_stage[i] = next_stage("f_stage%d" % i, J * NF)
-            cols = (slice(0, 2 * NF), slice(2 * NF, 3 * NF))[part]
-            out = f_stage[i][:, cols].bitcast(F32).rearrange("p (j x u) -> p j x u", x=P, u=2)
-            eng(out=out, in_=word_ps[i][part][:].rearrange("p j u x -> p j x u"))
+        operator_parts = (slice(0, 2), slice(2, 3))
+
+        def group_words(i, copy):
+            staged["f", i] = next_stage("f_stage%d" % i, J * NF)
+            for bank, part in zip(word_ps[i], operator_parts):
+                out = staged["f", i][:, part.start * NF : part.stop * NF].bitcast(F32).rearrange("p (j x u) -> p j x u", x=P, u=2)
+                copy(out=out, in_=bank[:].rearrange("p j u x -> p j x u"))
 
         def quantize_f(i):
             f_mx[i] = mx_pair("f%d" % i, [J * P], "f%d" % (i % 2))
-            quantize(f_mx[i], (every, slice(0, 2 * P)), f_stage[i][:, 0 : 2 * NF], E5M2)
-            quantize(f_mx[i], (every, slice(2 * P, 3 * P)), f_stage[i][:, 2 * NF : 3 * NF], E5M2)
+            for part in operator_parts:
+                quantize(f_mx[i], (every, slice(part.start * P, part.stop * P)), staged["f", i][:, part.start * NF : part.stop * NF], E5M2)
 
         def dw_product(i):
             for j in range(J):
                 dw_ps[i, j] = next_bank("dw_ps%d%d" % (i, j), [N], F32)
-                mx_pass(dw_ps[i, j][:], f_mx[i], (every, slice(j * P, (j + 1) * P)), E5M2, x_mx, (every, i // PACK, every), E4M3, True, True)
+                mx_pass(dw_ps[i, j][:], f_mx[i], (every, slice(j * P, (j + 1) * P)), e4m3_mx["x"], (every, i // PACK, every), True, True)
 
-        def dw_out(i, j, eng):
-            if j == 0:
-                dw_sb[i] = sbuf("dw_sb%d" % i, [2, J * N], F32, "big%d" % ((1 + i) % 3))
-            eng(out=dw_sb[i][:, 0, j * N : (j + 1) * N], in_=dw_ps[i, j][:])
+        def dw_out(i, copies=(on_scalar, on_scalar, on_scalar)):
+            dw_sb[i] = sbuf("dw_sb%d" % i, [2, J * N], F32, "big%d" % ((1 + i) % BIG_BUFS))
+            for j in range(J):
+                copies[j](out=dw_sb[i][:, 0, j * N : (j + 1) * N], in_=dw_ps[i, j][:])
 
-        def dw_store(i, eng=nc.vector.tensor_copy):
-            eng(
-                out=dw_sb[i][:, 1, :].rearrange("p (c i j) -> p c j i", i=4, j=J), in_=dw_sb[i][:, 0, :].rearrange("p (j c i) -> p c j i", j=J, i=4)
+        def dw_store(i):
+            on_vector(
+                out=dw_sb[i][:, 1, :].rearrange("p (c i j) -> p c j i", i=4, j=J),
+                in_=dw_sb[i][:, 0, :].rearrange("p (j c i) -> p c j i", j=J, i=4),
             )
             nc.sync.dma_start(out=dw_hbm[i // PACK, i % PACK], in_=dw_sb[i][:, 1, :])
 
-        def group_m(b, j, u, eng):
-            key = "m%d%d%d" % (b, j, u)
-            staged[key] = next_stage("st_" + key, 2 * NF)
-            eng(
-                out=staged[key][:].rearrange("p (e y i t) -> p y e i t", e=2, i=4, t=PACK),
-                in_=dx_bf[b, j][:, :, u * 256 : (u + 1) * 256].rearrange("p t (y i e) -> p y e i t", i=4, e=2),
+        def step(i, copy_words=on_scalar, copy_dw=(on_scalar, on_scalar, on_scalar)):
+            first_product(i)
+            turn_words(i - 1)
+            if i >= 2:
+                dw_product(i - 2)
+            round_dx(i)
+            group_words(i - 1, copy_words)
+            if i >= 2:
+                dw_out(i - 2, copy_dw)
+
+        m_mx, dxo_ps = {}, {}
+        dxo_hbm = out_0.rearrange("b (p c) n -> b c p n", c=PACK)
+        dxo_places = ("relu0", "relu1", "relu2", "g_turned0", "g_turned1", "gate0", "gate1", "g0")
+
+        def group_m(b, j, u, copy):
+            staged["m", b, j, u] = next_stage("m_stage%d%d%d" % (b, j, u), PACK * HALF)
+            copy(
+                out=staged["m", b, j, u][:].rearrange("p (e y i t) -> p y e i t", e=2, i=4, t=PACK),
+                in_=dx_bf[b, j][:, :, u * HALF : (u + 1) * HALF].rearrange("p t (y i e) -> p y e i t", i=4, e=2),
             )
 
         def quantize_m(b, j, u):
             if (j, u) == (0, 0):
-                m_mx[b] = mx_pair("m%d" % b, [J, NF], "m" if b == 0 else "wc")
-            quantize(m_mx[b], (every, j, slice(u * 256, (u + 1) * 256)), staged["m%d%d%d" % (b, j, u)][:], E5M2)
+                m_mx[b] = mx_pair("m%d" % b, [J, NF], ("m", "wc")[b])
+            quantize(m_mx[b], (every, j, slice(u * HALF, (u + 1) * HALF)), staged["m", b, j, u][:], E5M2)
 
-        dxo_ps = {}
-
-        def dx_tiles(b, u):
+        def dx_product(b, u):
             for j in range(J):
                 for c in (2 * u, 2 * u + 1):
                     if j == 0:
                         dxo_ps[b, c] = next_bank("dxo_ps%d%d" % (b, c), [N], F32)
-                    mx_pass(dxo_ps[b, c][:], m_mx[b], (every, j, slice(c * P, (c + 1) * P)), E5M2, w_mx, (every, b, j, every), E4M3, j == 0, j == J - 1)
+                    features = (every, j, slice(c * P, (c + 1) * P))
+                    mx_pass(dxo_ps[b, c][:], m_mx[b], features, e4m3_mx["w"], (every, b, j, every), j == 0, j == J - 1)
 
-        def dx_store(b, c, eng):
-            res = sbuf("dxo%d%d" % (b, c), [N], F32, ("zm0", "zm1", "zm2", "g_t0", "g_t1", "gate0", "gate1", "g0")[b * PACK + c])
-            eng(out=res[:], in_=dxo_ps[b, c][:])
+        def dx_store(b, c, copy):
+            res = sbuf("dxo%d%d" % (b, c), [N], F32, dxo_places[b * PACK + c])
+            copy(out=res[:], in_=dxo_ps[b, c][:])
             nc.sync.dma_start(out=dxo_hbm[b, c], in_=res[:])
 
-        S = nc.scalar.copy
-        VC = nc.vector.tensor_copy
 
-        after_relu = {4: const_steps[0], 5: const_steps[2], 7: stat_steps[0]}
-        after_dot = {4: const_steps[1], 5: const_steps[3]}
-        relu_mask(0)
-        spread_mask()
-        sign_of(0)
-        transpose_g(0)
+        last = SLOTS - 1
+        run(input_levels[0])
+        run(input_levels[1])
+        relu_times_mask(0)
+        run(input_levels[2])
+        copy_mask_row()
+        open_gate(0)
+        turn_g(0)
         for k in range(1, SLOTS):
-            relu_mask(k)
-            if k < SLOTS - 1:
-                transpose_g(k)
-            sign_of(k)
-            sum_g(k - 1)
-            if k == SLOTS - 2:
-                transpose_g(k + 1)
-            if k in (4, 6):
-                group_wc(0, k // 6)
-            run(after_relu.get(k, []))
-            dot_g(k - 1)
-            run(after_dot.get(k, []))
-            if k == 6:
-                quantize_wc(0, 0)
-        sum_g(SLOTS - 1)
-        group_wc(0, 2)
-        run(stat_steps[1])
-        dot_g(SLOTS - 1)
-        turn["first"], turn["bank"] = 0, 2
-        group_wc(1, 2)
-        group_x(0)
-        group_w(0, 0)
-        group_w(0, 1)
-        quantize_wc(0, 1)
-        load_w(1)
-        run(stat_steps[2])
-        weigh_gate(0, 0)
-        run(stat_steps[3])
-        group_wc(1, 0)
-        weigh_gate(1, 0)
-        run(stat_steps[4])
-        quantize_wc(0, 2)
-        run(stat_steps[5])
-        weigh_gate(0, 1)
-        quantize_wc(1, 0)
-        for k in range(SLOTS):
-            affine_z(k, 0)
-            add_g(k, 0)
-            if k == 3:
-                fetch_grouped("wc12")
-                group_w(0, 2)
-                round_dz(0, 0)
-        group_wc(1, 1)
-        quantize_dz(0, 0)
-        fetch_grouped("x0")
-        group_x(1)
-        round_dz(1, 0)
-        fetch_grouped("w00")
-        group_w(1, 0)
-        quantize_wc(1, 2)
-        quantize_wc(1, 1)
-        fetch_grouped("w01")
-        quantize_dz(1, 0)
-        fetch_grouped("w02")
+            relu_times_mask(k)
+            if k < last:
+                turn_g(k)
+            open_gate(k)
+            sum_s1(k - 1)
+            if k == last - 1:
+                turn_g(last)
+            if k >= PACK and k % 2 == 0:
+                group_on_scalar("wc", 0, (k - PACK) // 2)
+            if k == 1:
+                run(input_levels[3])
+            sum_s2(k - 1)
+            if k == last - 1:
+                quantize_e4m3("wc", 0, 0)
+        sum_s1(last)
+        group_on_scalar("wc", 0, 2)
+        run(sum_levels[0])
+        sum_s2(last)
+        run(sum_levels[1])
 
-        def step(i, first=(S, S, S), words=(S, S), second=(S, S, S)):
-            if i < 8:
-                first_product(i)
-            if 1 <= i < 9:
-                turn_words(i - 1)
-            if 2 <= i:
-                dw_product(i - 2)
-            if i < 8:
-                for j in range(J):
-                    round_dx(i, j, first[j])
-            if 1 <= i < 9:
-                group_words(i - 1, 0, words[0])
-                group_words(i - 1, 1, words[1])
-            if 2 <= i:
-                for j in range(J):
-                    dw_out(i - 2, j, second[j])
+        turn["first_bank"], turn["bank"] = 0, HELD_BANKS
+        group_on_tensor("wc", 1, 2)
+        group_on_tensor("x", 0)
+        group_on_tensor("w", 0, 0)
+        group_on_tensor("w", 0, 1)
+        quantize_e4m3("wc", 0, 1)
+        load_w(1, "big0")
+        run(sum_levels[2])
+        weigh_gate(0, 0)
+        run(sum_levels[3])
+        group_on_scalar("wc", 1, 0)
+        weigh_gate(1, 0)
+        run(sum_levels[4])
+        quantize_e4m3("wc", 0, 2)
+        run(sum_levels[5])
+        weigh_gate(0, 1)
+        quantize_e4m3("wc", 1, 0)
+
+        ungated_dz(0, 0)
+        fetch_grouped("wc", 1, 2)
+        group_on_tensor("w", 0, 2)
+        round_dz(0, 0)
+        ungated_dz(1, 0)
+        group_on_scalar("wc", 1, 1)
+        quantize_dz(0, 0)
+        fetch_grouped("x", 0)
+        group_on_tensor("x", 1)
+        round_dz(1, 0)
+        fetch_grouped("w", 0, 0)
+        group_on_tensor("w", 1, 0)
+        quantize_e4m3("wc", 1, 2)
+        quantize_e4m3("wc", 1, 1)
+        fetch_grouped("w", 0, 1)
+        quantize_dz(1, 0)
+        fetch_grouped("w", 0, 2)
 
         first_product(0)
-        quantize_x(0)
-        quantize_w(0, 0)
+        quantize_e4m3("x", 0)
+        quantize_e4m3("w", 0, 0)
         weigh_gate(1, 1)
-        quantize_w(0, 1)
-        for k in range(PACK):
-            affine_z(k, 1)
-            add_g(k, 1)
-        for j in range(J):
-            round_dx(0, j, S)
-        quantize_w(0, 2)
+        quantize_e4m3("w", 0, 1)
+        ungated_dz(0, 1)
+        round_dx(0)
+        quantize_e4m3("w", 0, 2)
         round_dz(0, 1)
-        fetch_grouped("x1")
-        group_w(1, 1)
-        for k in range(PACK, SLOTS):
-            affine_z(k, 1)
-            add_g(k, 1)
-        fetch_grouped("w10")
+        fetch_grouped("x", 1)
+        group_on_tensor("w", 1, 1)
+        ungated_dz(1, 1)
+        fetch_grouped("w", 1, 0)
         quantize_dz(0, 1)
         step(1)
         round_dz(1, 1)
-        quantize_x(1)
+        quantize_e4m3("x", 1)
         quantize_f(0)
-        quantize_w(1, 0)
+        quantize_e4m3("w", 1, 0)
         quantize_dz(1, 1)
-        fetch_grouped("w11")
-        group_w(1, 2)
-        quantize_w(1, 1)
-        fetch_grouped("w12")
-        step(2, words=(VC, VC))
-        quantize_w(1, 2)
+        fetch_grouped("w", 1, 1)
+        group_on_tensor("w", 1, 2)
+        quantize_e4m3("w", 1, 1)
+        fetch_grouped("w", 1, 2)
+        step(2, copy_words=on_vector)
+        quantize_e4m3("w", 1, 2)
         quantize_f(1)
         dw_store(0)
-        step(3, words=(VC, VC))
+        step(3, copy_words=on_vector, copy_dw=(on_scalar, on_scalar, on_vector))
         quantize_f(2)
         dw_store(1)
-        for i in (4, 5):
+
+        for u in range(2):
+            i = PACK + u
             step(i)
-            u = i - 4
-            group_m(0, 0, u, VC)
-            group_m(0, 1, u, VC)
+            group_m(0, 0, u, on_vector)
+            group_m(0, 1, u, on_vector)
             quantize_f(i - 1)
             quantize_m(0, 0, u)
-            group_m(0, 2, u, VC)
+            group_m(0, 2, u, on_vector)
             quantize_m(0, 1, u)
             dw_store(i - 2)
             quantize_m(0, 2, u)
-            if u == 1:
-                dx_tiles(0, 0)
-                dx_store(0, 0, S)
-                dx_store(0, 1, VC)
-        step(6, words=(VC, VC))
-        quantize_f(5)
-        dx_tiles(0, 1)
-        dx_store(0, 2, VC)
-        dx_store(0, 3, VC)
-        dw_store(4)
-        step(7, first=(S, VC, S), words=(S, S))
-        turn_words(7)
-        group_m(1, 0, 0, VC)
-        quantize_f(6)
-        dw_product(6)
-        group_words(7, 0, VC)
-        group_words(7, 1, VC)
-        group_m(1, 1, 0, VC)
-        quantize_f(7)
-        dw_product(7)
-        dw_store(5)
-        for j in range(J):
-            dw_out(6, j, S)
+        for u in range(2):
+            i = UNITS - 2 + u
+            first_product(i)
+            dx_product(0, u)
+            round_dx(i)
+            dx_store(0, 2 * u, on_vector)
+            dx_store(0, 2 * u + 1, on_vector)
+            turn_words(i - 1)
+            dw_product(i - 2)
+            group_words(i - 1, (on_vector, on_scalar)[u])
+            dw_out(i - 2)
+            if u == 0:
+                quantize_f(i - 1)
+                dw_store(i - 2)
+
+        final = UNITS - 1
+        turn_words(final)
+        group_m(1, 0, 0, on_vector)
+        quantize_f(final - 1)
+        dw_product(final - 1)
+        group_words(final, on_vector)
+        group_m(1, 1, 0, on_vector)
+        quantize_f(final)
+        dw_product(final)
+        dw_store(final - 2)
+        dw_out(final - 1)
         quantize_m(1, 0, 0)
-        group_m(1, 2, 0, VC)
+        group_m(1, 2, 0, on_vector)
         quantize_m(1, 1, 0)
-        dw_store(6)
+        dw_store(final - 1)
         quantize_m(1, 2, 0)
-        for j in range(J):
-            dw_out(7, j, S)
-        dx_tiles(1, 0)
-        group_m(1, 1, 1, S)
-        group_m(1, 0, 1, VC)
-        dw_store(7)
-        group_m(1, 2, 1, S)
+        dw_out(final)
+        dx_product(1, 0)
+        group_m(1, 1, 1, on_scalar)
+        group_m(1, 0, 1, on_vector)
+        dw_store(final)
+        group_m(1, 2, 1, on_scalar)
         quantize_m(1, 0, 1)
         quantize_m(1, 1, 1)
-        dx_store(1, 0, VC)
+        dx_store(1, 0, on_vector)
         quantize_m(1, 2, 1)
-        dx_store(1, 1, S)
-        dx_tiles(1, 1)
-        dx_store(1, 2, S)
-        dx_store(1, 3, VC)
+        dx_store(1, 1, on_scalar)
+        dx_product(1, 1)
+        dx_store(1, 2, on_scalar)
+        dx_store(1, 3, on_vector)

from contextlib import ExitStack

import concourse.mybir as mybir
from concourse.masks import make_identity

BS, NF, N, J, NOUT = 2, 512, 512, 3, 512
FLOPS = 2 * BS * J * NF * N * (2 * NOUT + N + N)

F32 = mybir.dt.float32
BF16 = mybir.dt.bfloat16
U32 = mybir.dt.uint32
U8 = mybir.dt.uint8
E4M3 = mybir.dt.float8_e4m3fn_x4
E5M2 = mybir.dt.float8_e5m2_x4
ALU = mybir.AluOpType
ACT = mybir.ActivationFunctionType

P = 128
PACK = 4
CONVS = 2
SLOTS = CONVS * PACK
UNITS = BS * PACK
BANKS = 8
HELD_BANKS = 2
STAGES = 7
RELU_BUFS = 3
BIG_BUFS = 3
HALF = NF // 2


def tile_layer_simple_pa_v_kernel(
    tc, X, W, N_batch, mask, cv1_w, cv1_b, cv2_w, cv2_b, bn_gamma, bn_beta, z, mean, rstd, grad_out, out_0, out_1
):
    nc = tc.nc
    vec = nc.vector
    on_scalar = nc.scalar.copy
    on_vector = nc.vector.tensor_copy
    every = slice(None)

    with ExitStack() as ctx:
        sb = ctx.enter_context(tc.tile_pool(name="sb", bufs=1))
        ps = ctx.enter_context(tc.psum_pool(name="ps", bufs=1))
        ctx.enter_context(tc.manual_schedule())

        def sbuf(name, shape, dtype, place=None):
            return sb.tile([P] + shape, dtype, name=name, tag=place or name, align_bytes=64)

        def psum(name, shape, dtype, bank):
            return ps.tile([P] + shape, dtype, name=name, tag="bank%d" % bank)

        turn = {"bank": 0, "first_bank": HELD_BANKS, "stage": 0}

        def next_bank(name, shape, dtype):
            bank = turn["first_bank"] + turn["bank"] % (BANKS - turn["first_bank"])
            turn["bank"] = turn["bank"] + 1
            return psum(name, shape, dtype, bank)

        def next_stage(name, width):
            place = "stage%d" % (turn["stage"] % STAGES)
            turn["stage"] = turn["stage"] + 1
            return sbuf(name, [width], BF16, place)

        def mx_pair(name, shape, place=None):
            place = place or name
            return sbuf(name + "_codes", shape, U32, place + "_c"), sbuf(name + "_scales", shape, U8, place + "_s")

        def quantize(pair, where, src, fmt):
            vec.quantize_mx(out=pair[0][where].bitcast(fmt), scales=pair[1][where], in_=src)

        def mx_pass(out, grad, grad_at, other, other_at, start, stop):
            nc.tensor.matmul_mx(
                out=out,
                lhsT=grad[0][grad_at].bitcast(E5M2),
                lhsT_scale=grad[1][grad_at],
                rhs=other[0][other_at].bitcast(E4M3),
                rhs_scale=other[1][other_at],
                start=start,
                stop=stop,
            )

        def run(calls):
            for call in calls:
                call()

        ident_f32 = sbuf("ident_f32", [P], F32)
        make_identity(nc, ident_f32[:])
        ident_bf = sbuf("ident_bf", [P], BF16)
        make_identity(nc, ident_bf[:])

        z_hbm = z.rearrange("b (g p s) m -> g s p b m", g=CONVS, s=PACK)
        g_hbm = grad_out.rearrange("b (g p h s) m -> g h p b s m", g=CONVS, h=2, s=2)
        wc_hbm = [w.rearrange("(p s) f -> p s f", s=PACK) for w in (cv2_w, cv1_w)]
        z_conv = [sbuf("z%d" % g, [PACK, BS, N], F32) for g in range(CONVS)]
        z_sb, g_sb, wc_raw, w_raw, x_raw = {}, {}, {}, {}, {}

        def load_z(k):
            z_sb[k] = z_conv[k // PACK][:, k % PACK, :, :]
            nc.sync.dma_start(out=z_sb[k], in_=z_hbm[k // PACK, k % PACK])

        def load_g_pair(k):
            pair = sbuf("g%d" % k, [BS, 2, N], BF16)
            nc.sync.dma_start(out=pair[:], in_=g_hbm[k // PACK, (k % PACK) // 2])
            g_sb[k], g_sb[k + 1] = pair[:, :, 0, :], pair[:, :, 1, :]

        def load_wc(g, j):
            if j == 0:
                wc_raw[g] = sbuf("wc_raw%d" % g, [PACK, J * NF], BF16, "big%d" % g)
            cols = slice(j * NF, (j + 1) * NF)
            nc.sync.dma_start(out=wc_raw[g][:, :, cols], in_=wc_hbm[g][:, :, cols])

        def load_x(b):
            x_raw[b] = sbuf("x_raw%d" % b, [PACK, N], BF16)
            nc.sync.dma_start(out=x_raw[b][:], in_=X[b].rearrange("(p t) n -> p t n", t=PACK))

        def load_w(b, place):
            w_raw[b] = sbuf("w_raw%d" % b, [PACK, N * J], BF16, place)
            nc.sync.dma_start(out=w_raw[b][:], in_=W[b].rearrange("(p t) n j -> p t (n j)", t=PACK))

        mask_col = sbuf("mask_col", [2 * BS, 2], BF16)
        nc.sync.dma_start(out=mask_col[:], in_=mask.rearrange("b o (h w e) -> w (b o h) e", h=2, e=2))
        load_z(0)
        gamma_sb = sbuf("gamma_sb", [CONVS, PACK], BF16)
        mean_sb = sbuf("mean_sb", [CONVS, PACK], F32)
        rstd_sb = sbuf("rstd_sb", [CONVS, PACK], F32)
        count_sb = sbuf("count_sb", [BS], BF16)
        nc.scalar.dma_start(out=count_sb[:], in_=N_batch.partition_broadcast(P))
        for tile, vector in ((rstd_sb, rstd), (gamma_sb, bn_gamma), (mean_sb, mean)):
            nc.scalar.dma_start(out=tile[:], in_=vector.rearrange("(g p s) -> p g s", g=CONVS, s=PACK))
        load_z(1)
        load_g_pair(0)
        for pair in range(1, SLOTS // 2):
            load_z(2 * pair)
            load_g_pair(2 * pair)
            load_z(2 * pair + 1)
            load_wc(0, pair - 1)
        for j in range(J):
            load_wc(1, j)
        load_x(0)
        load_w(0, "big2")
        load_x(1)

        def mask_row_in(tile):
            words = mask_col[:].rearrange("p k e -> p (k e)").bitcast(F32)
            for blk in range(2 * BS):
                nc.tensor.transpose(tile[:, blk, :], words[:, blk : blk + 1].to_broadcast([P, P]), ident_f32[:])
            return tile[:].rearrange("p k w -> p (k w)").bitcast(BF16)

        mask_row_ps = mask_row_in(psum("mask_ps", [2 * BS, P], F32, 0))
        mask_row = sbuf("mask_row", [BS * N], BF16)
        s0 = sbuf("s0", [1], F32)

        def copy_mask_row():
            row = mask_row_in(next_bank("mask_ps2", [2 * BS, P], F32))
            nc.scalar.activation(out=mask_row[:], in_=row, func=ACT.Identity, accum_out=s0[:])

        s3 = sbuf("s3", [SLOTS], F32)
        s2 = sbuf("s2", [SLOTS], F32)
        s1 = psum("s1", [SLOTS], F32, 1)
        gate = [sbuf("gate%d" % g, [BS, PACK, N], BF16) for g in range(CONVS)]
        s2_terms = sbuf("s2_terms", [BS, N], F32, "dx_b0_j2")
        relu_m, g_turned = {}, {}

        def relu_times_mask(k):
            relu_m[k] = sbuf("relu_m%d" % k, [BS, N], F32, "relu%d" % (k % RELU_BUFS))
            vec.scalar_tensor_tensor(
                out=relu_m[k][:].rearrange("p b m -> p (b m)"),
                in0=z_sb[k].rearrange("p b m -> p (b m)"),
                scalar=0.0,
                in1=mask_row_ps,
                op0=ALU.max,
                op1=ALU.mult,
                accum_out=s3[:, k : k + 1],
            )

        def open_gate(k):
            nc.scalar.activation(out=gate[k // PACK][:, :, k % PACK, :], in_=relu_m[k][:], func=ACT.Sign)

        def sum_s2(k):
            vec.scalar_tensor_tensor(
                out=s2_terms[:], in0=relu_m[k][:], scalar=1.0, in1=g_sb[k], op0=ALU.mult, op1=ALU.mult, accum_out=s2[:, k : k + 1]
            )

        def turn_g(k):
            bank = next_bank("g_ps%d" % k, [2 * BS, P], F32)
            for blk in range(2 * BS):
                b, h = divmod(blk, 2)
                nc.tensor.transpose(bank[:, blk, :], g_sb[k][:, b, :].bitcast(F32)[:, h * P : (h + 1) * P], ident_f32[:])
            g_turned[k] = sbuf("g_turned%d" % k, [2 * BS, P, 2], BF16, "g_turned%d" % (k % 2))
            on_scalar(out=g_turned[k][:].rearrange("p k c e -> p (k c e)").bitcast(F32), in_=bank[:].rearrange("p k c -> p (k c)"))

        def sum_s1(k):
            last = 4 * BS - 1
            for term in range(last + 1):
                blk, e = divmod(term, 2)
                nc.tensor.matmul(
                    s1[:, k : k + 1], lhsT=g_turned[k][:, blk, :, e], rhs=mask_col[:, blk, e : e + 1], start=(term == 0), stop=(term == last)
                )

        gamma_c = gamma_sb[:].rearrange("p g s -> p (g s)")
        mean_c = mean_sb[:].rearrange("p g s -> p (g s)")
        rstd_c = rstd_sb[:].rearrange("p g s -> p (g s)")
        total, inv_total = sbuf("total", [1], F32), sbuf("inv_total", [1], F32)
        coef_a, a_per_total, neg_rstd_sq, neg_b_factor = (
            sbuf(name, [SLOTS], F32) for name in ("coef_a", "a_per_total", "neg_rstd_sq", "neg_b_factor")
        )
        neg_rest, mean_s1, centred_s2, neg_level, a_s1, b_level, neg_b, coef_c = (
            sbuf(name, [SLOTS], F32) for name in ("neg_rest", "mean_s1", "centred_s2", "neg_level", "a_s1", "b_level", "neg_b", "coef_c")
        )
        input_levels = [
            [
                lambda: vec.tensor_reduce(out=total[:], in_=count_sb[:], axis=mybir.AxisListType.X, op=ALU.add),
                lambda: vec.tensor_tensor(out=coef_a[:], in0=rstd_c, in1=gamma_c, op=ALU.mult),
                lambda: vec.scalar_tensor_tensor(out=neg_rstd_sq[:], in0=rstd_c, scalar=-1.0, in1=rstd_c, op0=ALU.mult, op1=ALU.mult),
            ],
            [lambda: vec.reciprocal(out=inv_total[:], in_=total[:])],
            [lambda: vec.tensor_scalar(out=a_per_total[:], in0=coef_a[:], scalar1=inv_total[:], scalar2=None, op0=ALU.mult)],
            [lambda: vec.tensor_tensor(out=neg_b_factor[:], in0=neg_rstd_sq[:], in1=a_per_total[:], op=ALU.mult)],
        ]
        sum_levels = [
            [lambda: vec.scalar_tensor_tensor(out=neg_rest[:], in0=mean_c, scalar=s0[:], in1=s3[:], op0=ALU.mult, op1=ALU.subtract)],
            [
                lambda: vec.tensor_tensor(out=mean_s1[:], in0=mean_c, in1=s1[:], op=ALU.mult),
                lambda: vec.tensor_tensor(out=a_s1[:], in0=a_per_total[:], in1=s1[:], op=ALU.mult),
                lambda: vec.scalar_tensor_tensor(
                    out=neg_level[:], in0=neg_rest[:], scalar=inv_total[:], in1=mean_c, op0=ALU.mult, op1=ALU.subtract
                ),
            ],
            [lambda: vec.tensor_tensor(out=centred_s2[:], in0=s2[:], in1=mean_s1[:], op=ALU.subtract)],
            [lambda: vec.tensor_tensor(out=neg_b[:], in0=centred_s2[:], in1=neg_b_factor[:], op=ALU.mult)],
            [lambda: vec.tensor_tensor(out=b_level[:], in0=neg_b[:], in1=neg_level[:], op=ALU.mult)],
            [lambda: vec.tensor_tensor(out=coef_c[:], in0=b_level[:], in1=a_s1[:], op=ALU.subtract)],
        ]

        staged = {}
        dz_mx = mx_pair("dz", [BS, CONVS, N])

        def weigh_gate(g, b):
            row = mask_row[:, b * N : (b + 1) * N].unsqueeze(1).to_broadcast([P, PACK, N])
            vec.tensor_tensor(out=gate[g][:, b, :, :], in0=gate[g][:, b, :, :], in1=row, op=ALU.mult)

        def ungated_dz(g, b):
            for k in range(g * PACK, (g + 1) * PACK):
                here, col = z_sb[k][:, b, :], slice(k, k + 1)
                nc.scalar.activation(out=here, in_=here, func=ACT.Identity, scale=neg_b[:, col], bias=coef_c[:, col])
                vec.scalar_tensor_tensor(out=here, in0=g_sb[k][:, b, :], scalar=coef_a[:, col], in1=here, op0=ALU.mult, op1=ALU.add)

        def round_dz(g, b):
            staged["dz", g, b] = next_stage("dz_stage%d%d" % (g, b), PACK * N)
            vec.tensor_tensor(
                out=staged["dz", g, b][:].rearrange("p (t x s) -> p x s t", t=PACK, s=PACK),
                in0=z_conv[g][:, :, b, :].rearrange("p s (x t) -> p x s t", t=PACK),
                in1=gate[g][:, b, :, :].rearrange("p s (x t) -> p x s t", t=PACK),
                op=ALU.mult,
            )

        def quantize_dz(g, b):
            quantize(dz_mx, (every, b, g, every), staged["dz", g, b][:], E5M2)

        e4m3_mx = {"wc": mx_pair("wc", [CONVS, J, NF]), "w": mx_pair("w", [BS, J, N]), "x": mx_pair("x", [BS, N])}
        grouped_ps = {}

        def raw_rows(key):
            if key[0] == "wc":
                return wc_raw[key[1]][:, :, key[2] * NF : (key[2] + 1) * NF]
            if key[0] == "x":
                return x_raw[key[1]][:]
            return w_raw[key[1]][:].rearrange("p t (n j) -> p j t n", j=J)[:, key[2], :, :]

        def key_name(key):
            return "_".join(str(part) for part in key)

        def group_on_scalar(*key):
            staged[key] = next_stage("st_" + key_name(key), PACK * N)
            on_scalar(
                out=staged[key][:].rearrange("p (c i t) -> p c t i", i=4, t=PACK), in_=raw_rows(key).rearrange("p t (c i) -> p c t i", i=4)
            )

        def group_on_tensor(*key):
            grouped_ps[key] = [next_bank("grp_%s_%d" % (key_name(key), half), [2, P, PACK], BF16) for half in range(2)]
            for q in range(N // P):
                nc.tensor.matmul(
                    grouped_ps[key][q // 2][:, q % 2, :, :].rearrange("p (c i) t -> p c t i", i=8),
                    lhsT=ident_bf[:],
                    rhs=raw_rows(key)[:, :, q * P : (q + 1) * P].rearrange("p t (c i) -> p c t i", i=8),
                    start=True,
                    stop=True,
                )

        def fetch_grouped(*key):
            staged[key] = next_stage("st_" + key_name(key), PACK * N)
            for half in range(2):
                cols = slice(half * 2 * N, (half + 1) * 2 * N)
                on_scalar(out=staged[key][:, cols], in_=grouped_ps[key][half][:].rearrange("p q c t -> p (q c t)"))

        def quantize_e4m3(*key):
            quantize(e4m3_mx[key[0]], (every,) + key[1:] + (every,), staged[key][:], E4M3)

        dx_ps, dx_bf, word_ps, f_mx, dw_ps, dw_sb = {}, {}, {}, {}, {}, {}
        dw_hbm = out_1.rearrange("b (p t) n j -> b t p (n j)", t=PACK)

        def first_product(i):
            b, t = divmod(i, PACK)
            for j in range(J):
                dx_ps[i, j] = next_bank("dx_ps%d%d" % (i, j), [NF], F32)
                for g in range(CONVS):
                    nodes = (every, b, g, slice(t * P, (t + 1) * P))
                    mx_pass(dx_ps[i, j][:], dz_mx, nodes, e4m3_mx["wc"], (every, g, j, every), g == 0, g == CONVS - 1)

        def round_dx(i):
            b, t = divmod(i, PACK)
            for j in range(J):
                if t == 0:
                    dx_bf[b, j] = sbuf("dx_bf%d%d" % (b, j), [PACK, NF], BF16, "dx_b%d_j%d" % (b, j))
                out = dx_bf[b, j][:, t, :].rearrange("p (u w e) -> p u w e", u=2, e=2)
                on_scalar(out=out, in_=dx_ps[i, j][:].rearrange("p (w u e) -> p u w e", u=2, e=2))

        def turn_words(i):
            b, t = divmod(i, PACK)
            word_ps[i] = [next_bank("word_ps%d_0" % i, [2, 2, P], F32), next_bank("word_ps%d_1" % i, [1, 2, P], F32)]
            for j in range(J):
                words = dx_bf[b, j][:, t, :].bitcast(F32)
                for u in range(2):
                    nc.tensor.transpose(word_ps[i][j // 2][:, j % 2, u, :], words[:, u * P : (u + 1) * P], ident_f32[:])

        operator_parts = (slice(0, 2), slice(2, 3))

        def group_words(i, copy):
            staged["f", i] = next_stage("f_stage%d" % i, J * NF)
            for bank, part in zip(word_ps[i], operator_parts):
                out = staged["f", i][:, part.start * NF : part.stop * NF].bitcast(F32).rearrange("p (j x u) -> p j x u", x=P, u=2)
                copy(out=out, in_=bank[:].rearrange("p j u x -> p j x u"))

        def quantize_f(i):
            f_mx[i] = mx_pair("f%d" % i, [J * P], "f%d" % (i % 2))
            for part in operator_parts:
                quantize(f_mx[i], (every, slice(part.start * P, part.stop * P)), staged["f", i][:, part.start * NF : part.stop * NF], E5M2)

        def dw_product(i):
            for j in range(J):
                dw_ps[i, j] = next_bank("dw_ps%d%d" % (i, j), [N], F32)
                mx_pass(dw_ps[i, j][:], f_mx[i], (every, slice(j * P, (j + 1) * P)), e4m3_mx["x"], (every, i // PACK, every), True, True)

        def dw_out(i, copies=(on_scalar, on_scalar, on_scalar)):
            dw_sb[i] = sbuf("dw_sb%d" % i, [2, J * N], F32, "big%d" % ((1 + i) % BIG_BUFS))
            for j in range(J):
                copies[j](out=dw_sb[i][:, 0, j * N : (j + 1) * N], in_=dw_ps[i, j][:])

        def dw_store(i):
            on_vector(
                out=dw_sb[i][:, 1, :].rearrange("p (c i j) -> p c j i", i=4, j=J),
                in_=dw_sb[i][:, 0, :].rearrange("p (j c i) -> p c j i", j=J, i=4),
            )
            nc.sync.dma_start(out=dw_hbm[i // PACK, i % PACK], in_=dw_sb[i][:, 1, :])

        def step(i, copy_words=on_scalar, copy_dw=(on_scalar, on_scalar, on_scalar)):
            first_product(i)
            turn_words(i - 1)
            if i >= 2:
                dw_product(i - 2)
            round_dx(i)
            group_words(i - 1, copy_words)
            if i >= 2:
                dw_out(i - 2, copy_dw)

        m_mx, dxo_ps = {}, {}
        dxo_hbm = out_0.rearrange("b (p c) n -> b c p n", c=PACK)
        dxo_places = ("relu0", "relu1", "relu2", "g_turned0", "g_turned1", "gate0", "gate1", "g0")

        def group_m(b, j, u, copy):
            staged["m", b, j, u] = next_stage("m_stage%d%d%d" % (b, j, u), PACK * HALF)
            copy(
                out=staged["m", b, j, u][:].rearrange("p (e y i t) -> p y e i t", e=2, i=4, t=PACK),
                in_=dx_bf[b, j][:, :, u * HALF : (u + 1) * HALF].rearrange("p t (y i e) -> p y e i t", i=4, e=2),
            )

        def quantize_m(b, j, u):
            if (j, u) == (0, 0):
                m_mx[b] = mx_pair("m%d" % b, [J, NF], ("m", "wc")[b])
            quantize(m_mx[b], (every, j, slice(u * HALF, (u + 1) * HALF)), staged["m", b, j, u][:], E5M2)

        def dx_product(b, u):
            for j in range(J):
                for c in (2 * u, 2 * u + 1):
                    if j == 0:
                        dxo_ps[b, c] = next_bank("dxo_ps%d%d" % (b, c), [N], F32)
                    features = (every, j, slice(c * P, (c + 1) * P))
                    mx_pass(dxo_ps[b, c][:], m_mx[b], features, e4m3_mx["w"], (every, b, j, every), j == 0, j == J - 1)

        def dx_store(b, c, copy):
            res = sbuf("dxo%d%d" % (b, c), [N], F32, dxo_places[b * PACK + c])
            copy(out=res[:], in_=dxo_ps[b, c][:])
            nc.sync.dma_start(out=dxo_hbm[b, c], in_=res[:])


        last = SLOTS - 1
        run(input_levels[0])
        run(input_levels[1])
        relu_times_mask(0)
        run(input_levels[2])
        copy_mask_row()
        open_gate(0)
        turn_g(0)
        for k in range(1, SLOTS):
            relu_times_mask(k)
            if k < last:
                turn_g(k)
            open_gate(k)
            sum_s1(k - 1)
            if k == last - 1:
                turn_g(last)
            if k >= PACK and k % 2 == 0:
                group_on_scalar("wc", 0, (k - PACK) // 2)
            if k == 1:
                run(input_levels[3])
            sum_s2(k - 1)
            if k == last - 1:
                quantize_e4m3("wc", 0, 0)
        sum_s1(last)
        group_on_scalar("wc", 0, 2)
        run(sum_levels[0])
        sum_s2(last)
        run(sum_levels[1])

        turn["first_bank"], turn["bank"] = 0, HELD_BANKS
        group_on_tensor("wc", 1, 2)
        group_on_tensor("x", 0)
        group_on_tensor("w", 0, 0)
        group_on_tensor("w", 0, 1)
        quantize_e4m3("wc", 0, 1)
        load_w(1, "big0")
        run(sum_levels[2])
        weigh_gate(0, 0)
        run(sum_levels[3])
        group_on_scalar("wc", 1, 0)
        weigh_gate(1, 0)
        run(sum_levels[4])
        quantize_e4m3("wc", 0, 2)
        run(sum_levels[5])
        weigh_gate(0, 1)
        quantize_e4m3("wc", 1, 0)

        ungated_dz(0, 0)
        fetch_grouped("wc", 1, 2)
        group_on_tensor("w", 0, 2)
        round_dz(0, 0)
        ungated_dz(1, 0)
        group_on_scalar("wc", 1, 1)
        quantize_dz(0, 0)
        fetch_grouped("x", 0)
        group_on_tensor("x", 1)
        round_dz(1, 0)
        fetch_grouped("w", 0, 0)
        group_on_tensor("w", 1, 0)
        quantize_e4m3("wc", 1, 2)
        quantize_e4m3("wc", 1, 1)
        fetch_grouped("w", 0, 1)
        quantize_dz(1, 0)
        fetch_grouped("w", 0, 2)

        first_product(0)
        quantize_e4m3("x", 0)
        quantize_e4m3("w", 0, 0)
        weigh_gate(1, 1)
        quantize_e4m3("w", 0, 1)
        ungated_dz(0, 1)
        round_dx(0)
        quantize_e4m3("w", 0, 2)
        round_dz(0, 1)
        fetch_grouped("x", 1)
        group_on_tensor("w", 1, 1)
        ungated_dz(1, 1)
        fetch_grouped("w", 1, 0)
        quantize_dz(0, 1)
        step(1)
        round_dz(1, 1)
        quantize_e4m3("x", 1)
        quantize_f(0)
        quantize_e4m3("w", 1, 0)
        quantize_dz(1, 1)
        fetch_grouped("w", 1, 1)
        group_on_tensor("w", 1, 2)
        quantize_e4m3("w", 1, 1)
        fetch_grouped("w", 1, 2)
        step(2, copy_words=on_vector)
        quantize_e4m3("w", 1, 2)
        quantize_f(1)
        dw_store(0)
        step(3, copy_words=on_vector, copy_dw=(on_scalar, on_scalar, on_vector))
        quantize_f(2)
        dw_store(1)

        for u in range(2):
            i = PACK + u
            step(i)
            group_m(0, 0, u, on_vector)
            group_m(0, 1, u, on_vector)
            quantize_f(i - 1)
            quantize_m(0, 0, u)
            group_m(0, 2, u, on_vector)
            quantize_m(0, 1, u)
            dw_store(i - 2)
            quantize_m(0, 2, u)
        for u in range(2):
            i = UNITS - 2 + u
            first_product(i)
            dx_product(0, u)
            round_dx(i)
            dx_store(0, 2 * u, on_vector)
            dx_store(0, 2 * u + 1, on_vector)
            turn_words(i - 1)
            dw_product(i - 2)
            group_words(i - 1, (on_vector, on_scalar)[u])
            dw_out(i - 2)
            if u == 0:
                quantize_f(i - 1)
                dw_store(i - 2)

        final = UNITS - 1
        turn_words(final)
        group_m(1, 0, 0, on_vector)
        quantize_f(final - 1)
        dw_product(final - 1)
        group_words(final, on_vector)
        group_m(1, 1, 0, on_vector)
        quantize_f(final)
        dw_product(final)
        dw_store(final - 2)
        dw_out(final - 1)
        quantize_m(1, 0, 0)
        group_m(1, 2, 0, on_vector)
        quantize_m(1, 1, 0)
        dw_store(final - 1)
        quantize_m(1, 2, 0)
        dw_out(final)
        dx_product(1, 0)
        group_m(1, 1, 1, on_scalar)
        group_m(1, 0, 1, on_vector)
        dw_store(final)
        group_m(1, 2, 1, on_scalar)
        quantize_m(1, 0, 1)
        quantize_m(1, 1, 1)
        dx_store(1, 0, on_vector)
        quantize_m(1, 2, 1)
        dx_store(1, 1, on_scalar)
        dx_product(1, 1)
        dx_store(1, 2, on_scalar)
        dx_store(1, 3, on_vector)
